import numpy as np
import ml_dtypes


def mxq(x, axis, fmt="e4m3"):
    dtype, down = {"e4m3": (ml_dtypes.float8_e4m3fn, 7), "e5m2": (ml_dtypes.float8_e5m2, 14)}[fmt]
    v = np.moveaxis(np.asarray(x, np.float32).astype(ml_dtypes.bfloat16).astype(np.float64), axis, -1)
    blocks = v.reshape(v.shape[:-1] + (-1, 32))
    amax = np.abs(blocks).max(-1, keepdims=True)
    byte = np.maximum(np.where(amax > 0, np.frexp(amax)[1] - 1 + 127, 0) - down, 1)
    scale = np.exp2(byte - 127.0)
    codes = (blocks / scale).astype(np.float32).astype(dtype).astype(np.float64)
    return np.moveaxis((codes * scale).reshape(v.shape), -1, axis)


WIDE = False


def mx_kscale(k, group=512):
    if not WIDE:
        return np.ones(k)
    levels = np.array([20, -20, 10, -10, 0])
    if group != 512:
        return np.exp2(np.random.permutation(np.resize(levels, k // group))).repeat(group)
    a = np.random.permutation(np.resize(levels, k // 512 * 4)).reshape(k // 512, 4)
    idx = np.arange(k)
    return np.exp2(a[idx // 512, idx % 128 // 32])


BF16 = ml_dtypes.bfloat16


def bf(x):
    return np.asarray(x, np.float32).astype(BF16)


def f64(x):
    return np.asarray(x).astype(np.float64)


B, L, V, N = 2, 2048, 1024, 511


def _row_stats(w):
    norm = np.linalg.norm(w, axis=-1)
    r = np.where(norm > 1e-7, np.sinh(norm) / np.maximum(norm, 1e-7), 1.0)
    return r, np.cosh(norm)


def _safe_acosh(x):
    xm1 = np.maximum(x - 1.0, 0.0)
    near = xm1 < 1e-3
    taylor = np.sqrt(2.0 * np.maximum(xm1, 1e-12)) * (1.0 - xm1 / 12.0)
    exact = np.arccosh(np.maximum(x, 1.0 + 1e-7))
    return np.where(near, taylor, exact)


def _safe_acosh_prime(x):
    xm1 = np.maximum(x - 1.0, 0.0)
    near = xm1 < 1e-3
    root = np.sqrt(2.0 * np.maximum(xm1, 1e-12))
    taylor = np.where(xm1 > 1e-12, (1.0 - xm1 / 12.0) / root, 0.0) - root / 12.0
    taylor = np.where(x > 1.0, taylor, 0.0)
    xc = np.maximum(x, 1.0 + 1e-7)
    exact = 1.0 / np.sqrt(xc * xc - 1.0)
    return np.where(near, taylor, exact)


def setup_inputs():
    u = mx_kscale(V, group=32)
    u = u / np.max(u)
    m = np.random.standard_normal(N)
    sp = (np.random.standard_normal((B, L, N)) + np.random.uniform(-1.5, 1.5, (B, L, 1)) * m) / np.sqrt(N)
    t = np.sqrt(1.0 + np.sum(sp * sp, axis=-1, keepdims=True))
    h = bf(np.concatenate([t, sp], axis=-1))
    w0 = bf((np.random.standard_normal((V, N)) + np.random.uniform(-1.5, 1.5, (V, 1)) * m) * 0.7 / np.sqrt(N))
    ls = bf(0.6 + 0.1 * np.random.standard_normal(1))
    g = bf(np.random.standard_normal((B, L, V)) * np.exp2(np.random.randint(-12, 1, (B, L, 1))) * u)
    r, w_time = _row_stats(f64(w0))
    x = f64(h)[..., :1] * w_time - f64(h)[..., 1:] @ (r[:, None] * f64(w0)).T
    return {"hidden_states": h, "weight": bf(f64(w0) / u[:, None]), "logit_scale": ls,
            "x": np.asarray(x, np.float32), "r": np.asarray(r, np.float32), "w_time": np.asarray(w_time, np.float32),
            "grad_out": g}


def reference(hidden_states, weight, logit_scale, x, r, w_time, grad_out):
    xf = f64(x)
    tau = np.clip(f64(logit_scale), 0.01, 2.5)
    dx = f64(grad_out) * (-2.0 * tau * _safe_acosh(xf) * _safe_acosh_prime(xf))
    wl = np.concatenate([f64(w_time)[:, None], -f64(r)[:, None] * f64(weight)], axis=1)
    return mxq(dx, 2, "e5m2") @ mxq(wl, 0, "e4m3")

@@ -1,0 +1,273 @@
+from contextlib import ExitStack
+
+import concourse.mybir as mybir
+from concourse.masks import make_identity
+
+F32 = mybir.dt.float32
+BF16 = mybir.dt.bfloat16
+U32 = mybir.dt.uint32
+U8 = mybir.dt.uint8
+E5M2_X4 = mybir.dt.float8_e5m2_x4
+E4M3_X4 = mybir.dt.float8_e4m3fn_x4
+ALU = mybir.AluOpType
+FUNC = mybir.ActivationFunctionType
+
+P = 128
+PACK = 4
+K_PASS = P * PACK
+TOKENS = 4096
+VOCAB = 1024
+COLS = 512
+PASSES = VOCAB // K_PASS
+TILES = TOKENS // P
+CHUNK = 8
+CHUNKS = TILES // CHUNK
+UNITS = TILES * PASSES
+X_BANKS = 4
+X_PAIR = 2
+G_QUAD = 4
+BACKS_DURING_LOGS = 5
+
+FLOPS = 2 * TOKENS * VOCAB * COLS
+BYTES = TOKENS * VOCAB * (4 + 2) + VOCAB * (COLS - 1) * 2 + VOCAB * 8 + 2 + TOKENS * COLS * 4
+
+
+def tile_geodesiclmheadv2_t_v_kernel(
+    tc, hidden_states, weight, logit_scale, x, r, w_time, grad_out, out
+):
+    nc = tc.nc
+    x_view = x.flatten_outer_dims().rearrange("(c p n) v -> c p n v", p=P, n=CHUNK)
+    g_view = grad_out.flatten_outer_dims().rearrange("(c p n) v -> c p n v", p=P, n=CHUNK)
+    out_view = out.flatten_outer_dims().rearrange("(c p n) w -> c p n w", p=P, n=CHUNK)
+
+    with ExitStack() as stack:
+        keep = stack.enter_context(tc.tile_pool(name="keep", bufs=1))
+        x_pool = stack.enter_context(tc.tile_pool(name="x_pool", bufs=4))
+        g_pool = stack.enter_context(tc.tile_pool(name="g_pool", bufs=3))
+        sq_pool = stack.enter_context(tc.tile_pool(name="sq_pool", bufs=4))
+        long_pool = stack.enter_context(tc.tile_pool(name="long_pool", bufs=10))
+        mx_pool = stack.enter_context(tc.tile_pool(name="mx_pool", bufs=3))
+        xt_psum = stack.enter_context(tc.psum_pool(name="xt_psum", bufs=X_BANKS))
+        gt_psum = stack.enter_context(tc.psum_pool(name="gt_psum", bufs=2))
+        acc_psum = stack.enter_context(tc.psum_pool(name="acc_psum", bufs=2))
+        stack.enter_context(tc.manual_schedule())
+
+        x_tiles = {}
+        g_tiles = {}
+        xt_tiles = {}
+        gt_tiles = {}
+        e_tiles = {}
+        y_tiles = {}
+        dx_tiles = {}
+        code_tiles = {}
+        acc_tiles = {}
+        o_tiles = {}
+
+        def load_x(pair):
+            if pair * X_PAIR >= TILES:
+                return
+            first = pair * X_PAIR
+            c, n = divmod(first, CHUNK)
+            x_raw = x_pool.tile([P, X_PAIR, VOCAB], F32, name="x_raw")
+            nc.sync.dma_start(out=x_raw[:], in_=x_view[c, :, n : n + X_PAIR, :])
+            flat = x_raw[:].rearrange("p n v -> p (n v)")
+            nc.gpsimd.tensor_scalar(
+                out=flat, in0=flat, scalar1=1.0, scalar2=0.0, op0=ALU.max, op1=ALU.add
+            )
+            x_tiles[pair] = x_raw
+
+        def load_g(quad):
+            if quad * G_QUAD >= TILES:
+                return
+            c, n = divmod(quad * G_QUAD, CHUNK)
+            g_raw = g_pool.tile([P, G_QUAD, VOCAB], BF16, name="g_raw")
+            nc.sync.dma_start(out=g_raw[:], in_=g_view[c, :, n : n + G_QUAD, :])
+            g_tiles[quad] = g_raw
+
+        ls_sb = keep.tile([P, 1], BF16, name="ls_sb")
+        nc.sync.dma_start(out=ls_sb[:], in_=logit_scale.partition_broadcast(P))
+        r_sb = keep.tile([P, PASSES, PACK], F32, name="r_sb")
+        wt_sb = keep.tile([P, PASSES, PACK], F32, name="wt_sb")
+        with nc.allow_non_contiguous_dma(reason="16-byte runs of two small vectors"):
+            nc.sync.dma_start(out=r_sb[:], in_=r.rearrange("(g p j) -> p g j", p=P, j=PACK))
+            nc.sync.dma_start(out=wt_sb[:], in_=w_time.rearrange("(g p j) -> p g j", p=P, j=PACK))
+
+        ident_f32 = keep.tile([P, P], F32, name="ident_f32")
+        make_identity(nc, ident_f32[:])
+        ident_bf16 = keep.tile([P, P], BF16, name="ident_bf16")
+        make_identity(nc, ident_bf16[:])
+
+        load_x(0)
+        load_x(1)
+        w_raw = keep.tile([P, PASSES, PACK, COLS - 1], BF16, name="w_raw")
+        nc.sync.dma_start(
+            out=w_raw[:], in_=weight.rearrange("(g p j) w -> p g j w", p=P, j=PACK)
+        )
+        load_x(2)
+        load_x(3)
+        load_g(0)
+        load_g(1)
+        load_g(2)
+
+        warm = keep.tile([P, 1], F32, name="warm")
+        nc.vector.memset(warm[:], 1.0)
+        nc.scalar.activation(out=warm[:], in_=warm[:], func=FUNC.Abs_reciprocal_sqrt)
+
+        c_sb = keep.tile([P, 1], F32, name="c_sb")
+        nc.vector.tensor_scalar(
+            out=c_sb[:], in0=ls_sb[:], scalar1=0.01, scalar2=2.5, op0=ALU.max, op1=ALU.min
+        )
+        nc.vector.tensor_scalar_mul(out=c_sb[:], in0=c_sb[:], scalar1=-2.0)
+        neg_r = keep.tile([P, PASSES, PACK], F32, name="neg_r")
+        nc.vector.tensor_scalar_mul(out=neg_r[:], in0=r_sb[:], scalar1=-1.0)
+
+        w_grp = keep.tile([P, PASSES, COLS, PACK], BF16, name="w_grp", align_bytes=64)
+        w_codes = keep.tile([P, PASSES, COLS], U32, name="w_codes", align_bytes=64)
+        w_scales = keep.tile([P, PASSES, COLS], U8, name="w_scales", align_bytes=64)
+
+        def prepare_w(g):
+            nc.gpsimd.tensor_copy(out=w_grp[:, g, 0, :], in_=wt_sb[:, g, :])
+            nc.gpsimd.tensor_tensor(
+                out=w_grp[:, g, 1:COLS, :],
+                in0=w_raw[:, g].rearrange("p j w -> p w j"),
+                in1=neg_r[:, g, :].unsqueeze(1).to_broadcast([P, COLS - 1, PACK]),
+                op=ALU.mult,
+            )
+
+        def quantise_w(g):
+            nc.vector.quantize_mx(
+                out=w_codes[:, g, :].bitcast(E4M3_X4),
+                scales=w_scales[:, g, :],
+                in_=w_grp[:, g].rearrange("p w j -> p (w j)"),
+            )
+
+        prepare_w(0)
+        prepare_w(1)
+
+        def transpose_x(unit):
+            if unit >= UNITS:
+                return
+            i, g = divmod(unit, PASSES)
+            x_raw = x_tiles[i // X_PAIR]
+            cols = x_raw[:, i % X_PAIR, :].rearrange("p (g c j) -> p g j c", g=PASSES, j=PACK)
+            xt = xt_psum.tile([P, PACK, P], F32, name="xt")
+            for j in range(PACK):
+                nc.tensor.transpose(xt[:, j, :], cols[:, g, j, :], ident_f32[:])
+            xt_tiles[unit] = xt
+            if unit % (X_PAIR * PASSES) == X_PAIR * PASSES - 1:
+                load_x(i // X_PAIR + 4)
+
+        def front(unit):
+            i, g = divmod(unit, PASSES)
+            if g == 0:
+                e_tiles[i] = long_pool.tile([P, VOCAB], F32, name="e_sb")
+                y_tiles[i] = long_pool.tile([P, VOCAB], F32, name="y_sb")
+            half = slice(g * K_PASS, (g + 1) * K_PASS)
+            xt = xt_tiles.pop(unit)[:].rearrange("p j t -> p (j t)")
+            sq = sq_pool.tile([P, K_PASS], F32, name="sq")
+            nc.scalar.activation(out=sq[:], in_=xt, func=FUNC.Square)
+            nc.scalar.activation(
+                out=e_tiles[i][:, half], in_=sq[:], func=FUNC.Abs_reciprocal_sqrt, bias=-1.0
+            )
+            nc.vector.scalar_tensor_tensor(
+                out=sq[:], in0=sq[:], scalar=-1.0, in1=e_tiles[i][:, half],
+                op0=ALU.add, op1=ALU.mult,
+            )
+            nc.vector.tensor_tensor(out=y_tiles[i][:, half], in0=sq[:], in1=xt, op=ALU.add)
+            transpose_x(unit + X_BANKS)
+
+        def log(i):
+            nc.scalar.activation(out=y_tiles[i][:], in_=y_tiles[i][:], func=FUNC.Ln)
+
+        def transpose_g(i):
+            if i >= TILES:
+                return
+            g_raw = g_tiles[i // G_QUAD]
+            cols = g_raw[:, i % G_QUAD, :].rearrange("p (g c j) -> p g j c", g=PASSES, j=PACK)
+            gt = gt_psum.tile([P, PASSES, PACK, P], BF16, name="gt")
+            for g in range(PASSES):
+                for j in range(PACK):
+                    nc.tensor.transpose(gt[:, g, j, :], cols[:, g, j, :], ident_bf16[:])
+            gt_tiles[i] = gt
+            if i % G_QUAD == G_QUAD - 1:
+                load_g(i // G_QUAD + 3)
+
+        def back(i):
+            transpose_g(i + 1)
+            t_sb = y_tiles.pop(i)
+            nc.vector.scalar_tensor_tensor(
+                out=t_sb[:], in0=t_sb[:], scalar=c_sb[:, 0:1], in1=e_tiles.pop(i)[:],
+                op0=ALU.mult, op1=ALU.mult,
+            )
+            gt = gt_tiles.pop(i)
+            dx = mx_pool.tile([P, PASSES, P, PACK], BF16, name="dx", align_bytes=64)
+            for g in range(PASSES):
+                nc.vector.scalar_tensor_tensor(
+                    out=dx[:, g],
+                    in0=t_sb[:, g * K_PASS : (g + 1) * K_PASS].rearrange("p (j t) -> p t j", j=PACK),
+                    scalar=0.0,
+                    in1=gt[:, g].rearrange("p j t -> p t j"),
+                    op0=ALU.min, op1=ALU.mult,
+                )
+            dx_tiles[i] = dx
+            multiply(i - 1)
+            drain(i - 2)
+
+        def multiply(i):
+            if i < 0:
+                return
+            codes = mx_pool.tile([P, PASSES, P], U32, name="codes", align_bytes=64)
+            scales = mx_pool.tile([P, PASSES, P], U8, name="scales", align_bytes=64)
+            nc.vector.quantize_mx(
+                out=codes[:].rearrange("p g t -> p (g t)").bitcast(E5M2_X4),
+                scales=scales[:].rearrange("p g t -> p (g t)"),
+                in_=dx_tiles.pop(i)[:].rearrange("p g t j -> p (g t j)"),
+            )
+            acc = acc_psum.tile([P, COLS], F32, name="acc")
+            for g in range(PASSES):
+                nc.tensor.matmul_mx(
+                    out=acc[:],
+                    lhsT=codes[:, g, :].bitcast(E5M2_X4),
+                    lhsT_scale=scales[:, g, :],
+                    rhs=w_codes[:, g, :].bitcast(E4M3_X4),
+                    rhs_scale=w_scales[:, g, :],
+                    start=(g == 0),
+                    stop=(g == PASSES - 1),
+                )
+            acc_tiles[i] = acc
+
+        def drain(i):
+            if i < 0:
+                return
+            if i % 2 == 0:
+                o_tiles[i // 2] = mx_pool.tile([P, 2, COLS], F32, name="o_sb")
+            o_sb = o_tiles[i // 2]
+            nc.scalar.copy(out=o_sb[:, i % 2, :], in_=acc_tiles.pop(i)[:])
+            if i % 2 == 1:
+                c, n = divmod(i - 1, CHUNK)
+                nc.sync.dma_start(out=out_view[c, :, n : n + 2, :], in_=o_sb[:])
+
+        for unit in range(X_BANKS):
+            transpose_x(unit)
+        for unit in range(CHUNK * PASSES):
+            front(unit)
+        quantise_w(0)
+        quantise_w(1)
+        transpose_g(0)
+        for c in range(CHUNKS):
+            first = c * CHUNK
+            for n in range(CHUNK):
+                log(first + n)
+            for n in range(BACKS_DURING_LOGS):
+                back(first + n)
+            late = BACKS_DURING_LOGS
+            for n in range(CHUNK):
+                if c + 1 < CHUNKS:
+                    for g in range(PASSES):
+                        front((first + CHUNK + n) * PASSES + g)
+                if n % 2 == 1 and n >= 3:
+                    back(first + late)
+                    late += 1
+        multiply(TILES - 1)
+        drain(TILES - 2)
+        drain(TILES - 1)

@@ -22,7 +22,6 @@ PASSES = VOCAB // K_PASS
 TILES = TOKENS // P
 CHUNK = 8
 CHUNKS = TILES // CHUNK
-UNITS = TILES * PASSES
 X_BANKS = 4
 X_PAIR = 2
 G_QUAD = 4
@@ -44,7 +43,7 @@ def tile_geodesiclmheadv2_t_v_kernel(
         keep = stack.enter_context(tc.tile_pool(name="keep", bufs=1))
         x_pool = stack.enter_context(tc.tile_pool(name="x_pool", bufs=4))
         g_pool = stack.enter_context(tc.tile_pool(name="g_pool", bufs=3))
-        sq_pool = stack.enter_context(tc.tile_pool(name="sq_pool", bufs=4))
+        sq_pool = stack.enter_context(tc.tile_pool(name="sq_pool", bufs=3))
         long_pool = stack.enter_context(tc.tile_pool(name="long_pool", bufs=10))
         mx_pool = stack.enter_context(tc.tile_pool(name="mx_pool", bufs=3))
         xt_psum = stack.enter_context(tc.psum_pool(name="xt_psum", bufs=X_BANKS))
@@ -70,11 +69,18 @@ def tile_geodesiclmheadv2_t_v_kernel(
             c, n = divmod(first, CHUNK)
             x_raw = x_pool.tile([P, X_PAIR, VOCAB], F32, name="x_raw")
             nc.sync.dma_start(out=x_raw[:], in_=x_view[c, :, n : n + X_PAIR, :])
-            flat = x_raw[:].rearrange("p n v -> p (n v)")
-            nc.gpsimd.tensor_scalar(
-                out=flat, in0=flat, scalar1=1.0, scalar2=0.0, op0=ALU.max, op1=ALU.add
-            )
             x_tiles[pair] = x_raw
+
+        def clamp(pair):
+            if pair * X_PAIR >= TILES:
+                return
+            flat = x_tiles[pair][:].rearrange("p n v -> p (n v)")
+            if pair % 2 == 0:
+                nc.vector.tensor_scalar(
+                    out=flat, in0=flat, scalar1=1.0, scalar2=-1.0, op0=ALU.max, op1=ALU.add
+                )
+            else:
+                nc.scalar.activation(out=flat, in_=flat, func=FUNC.Relu, bias=-1.0)
 
         def load_g(quad):
             if quad * G_QUAD >= TILES:
@@ -144,40 +150,49 @@ def tile_geodesiclmheadv2_t_v_kernel(
         prepare_w(0)
         prepare_w(1)
 
-        def transpose_x(unit):
-            if unit >= UNITS:
+        def transpose_x(i):
+            if i >= TILES:
                 return
-            i, g = divmod(unit, PASSES)
             x_raw = x_tiles[i // X_PAIR]
             cols = x_raw[:, i % X_PAIR, :].rearrange("p (g c j) -> p g j c", g=PASSES, j=PACK)
-            xt = xt_psum.tile([P, PACK, P], F32, name="xt")
-            for j in range(PACK):
-                nc.tensor.transpose(xt[:, j, :], cols[:, g, j, :], ident_f32[:])
-            xt_tiles[unit] = xt
-            if unit % (X_PAIR * PASSES) == X_PAIR * PASSES - 1:
+            for g in range(PASSES):
+                xt = xt_psum.tile([P, PACK, P], F32, name="xt")
+                for j in range(PACK):
+                    nc.tensor.transpose(xt[:, j, :], cols[:, g, j, :], ident_f32[:])
+                xt_tiles[i, g] = xt
+            if i % X_PAIR == X_PAIR - 1:
                 load_x(i // X_PAIR + 4)
 
-        def front(unit):
-            i, g = divmod(unit, PASSES)
-            if g == 0:
-                e_tiles[i] = long_pool.tile([P, VOCAB], F32, name="e_sb")
-                y_tiles[i] = long_pool.tile([P, VOCAB], F32, name="y_sb")
-            half = slice(g * K_PASS, (g + 1) * K_PASS)
-            xt = xt_tiles.pop(unit)[:].rearrange("p j t -> p (j t)")
-            sq = sq_pool.tile([P, K_PASS], F32, name="sq")
-            nc.scalar.activation(out=sq[:], in_=xt, func=FUNC.Square)
-            nc.scalar.activation(
-                out=e_tiles[i][:, half], in_=sq[:], func=FUNC.Abs_reciprocal_sqrt, bias=-1.0
-            )
-            nc.vector.scalar_tensor_tensor(
-                out=sq[:], in0=sq[:], scalar=-1.0, in1=e_tiles[i][:, half],
-                op0=ALU.add, op1=ALU.mult,
-            )
-            nc.vector.tensor_tensor(out=y_tiles[i][:, half], in0=sq[:], in1=xt, op=ALU.add)
-            transpose_x(unit + X_BANKS)
+        def front(i):
+            e_sb = long_pool.tile([P, PASSES, K_PASS], F32, name="e_sb")
+            y_sb = long_pool.tile([P, PASSES, K_PASS], F32, name="y_sb")
+            sq = sq_pool.tile([P, PASSES, K_PASS], F32, name="sq")
+            ut = [xt_tiles.pop((i, g))[:].rearrange("p j t -> p (j t)") for g in range(PASSES)]
+            for g in range(PASSES):
+                nc.scalar.activation(out=sq[:, g], in_=ut[g], func=FUNC.Square, bias=1.0)
+            for g in range(PASSES):
+                nc.scalar.activation(
+                    out=e_sb[:, g], in_=sq[:, g], func=FUNC.Abs_reciprocal_sqrt, bias=-1.0
+                )
+            for g in range(PASSES):
+                nc.vector.scalar_tensor_tensor(
+                    out=sq[:, g], in0=sq[:, g], scalar=-1.0, in1=e_sb[:, g],
+                    op0=ALU.add, op1=ALU.mult,
+                )
+            for g in range(PASSES):
+                nc.vector.scalar_tensor_tensor(
+                    out=y_sb[:, g], in0=ut[g], scalar=1.0, in1=sq[:, g],
+                    op0=ALU.add, op1=ALU.add,
+                )
+            e_tiles[i] = e_sb
+            y_tiles[i] = y_sb
+            if (i + 3) % X_PAIR == 0:
+                clamp((i + 3) // X_PAIR)
+            transpose_x(i + 2)
 
         def log(i):
-            nc.scalar.activation(out=y_tiles[i][:], in_=y_tiles[i][:], func=FUNC.Ln)
+            flat = y_tiles[i][:].rearrange("p g k -> p (g k)")
+            nc.scalar.activation(out=flat, in_=flat, func=FUNC.Ln)
 
         def transpose_g(i):
             if i >= TILES:
@@ -195,16 +210,18 @@ def tile_geodesiclmheadv2_t_v_kernel(
         def back(i):
             transpose_g(i + 1)
             t_sb = y_tiles.pop(i)
-            nc.vector.scalar_tensor_tensor(
-                out=t_sb[:], in0=t_sb[:], scalar=c_sb[:, 0:1], in1=e_tiles.pop(i)[:],
-                op0=ALU.mult, op1=ALU.mult,
-            )
+            e_sb = e_tiles.pop(i)
+            for g in range(PASSES):
+                nc.vector.scalar_tensor_tensor(
+                    out=t_sb[:, g], in0=t_sb[:, g], scalar=c_sb[:, 0:1], in1=e_sb[:, g],
+                    op0=ALU.mult, op1=ALU.mult,
+                )
             gt = gt_tiles.pop(i)
             dx = mx_pool.tile([P, PASSES, P, PACK], BF16, name="dx", align_bytes=64)
             for g in range(PASSES):
                 nc.vector.scalar_tensor_tensor(
                     out=dx[:, g],
-                    in0=t_sb[:, g * K_PASS : (g + 1) * K_PASS].rearrange("p (j t) -> p t j", j=PACK),
+                    in0=t_sb[:, g].rearrange("p (j t) -> p t j", j=PACK),
                     scalar=0.0,
                     in1=gt[:, g].rearrange("p j t -> p t j"),
                     op0=ALU.min, op1=ALU.mult,
@@ -247,10 +264,12 @@ def tile_geodesiclmheadv2_t_v_kernel(
                 c, n = divmod(i - 1, CHUNK)
                 nc.sync.dma_start(out=out_view[c, :, n : n + 2, :], in_=o_sb[:])
 
-        for unit in range(X_BANKS):
-            transpose_x(unit)
-        for unit in range(CHUNK * PASSES):
-            front(unit)
+        clamp(0)
+        transpose_x(0)
+        transpose_x(1)
+        clamp(1)
+        for i in range(CHUNK):
+            front(i)
         quantise_w(0)
         quantise_w(1)
         transpose_g(0)
@@ -263,8 +282,7 @@ def tile_geodesiclmheadv2_t_v_kernel(
             late = BACKS_DURING_LOGS
             for n in range(CHUNK):
                 if c + 1 < CHUNKS:
-                    for g in range(PASSES):
-                        front((first + CHUNK + n) * PASSES + g)
+                    front(first + CHUNK + n)
                 if n % 2 == 1 and n >= 3:
                     back(first + late)
                     late += 1

@@ -22,10 +22,9 @@ PASSES = VOCAB // K_PASS
 TILES = TOKENS // P
 CHUNK = 8
 CHUNKS = TILES // CHUNK
-X_BANKS = 4
-X_PAIR = 2
 G_QUAD = 4
-BACKS_DURING_LOGS = 5
+O_PAIR = 2
+LEAD = 2
 
 FLOPS = 2 * TOKENS * VOCAB * COLS
 BYTES = TOKENS * VOCAB * (4 + 2) + VOCAB * (COLS - 1) * 2 + VOCAB * 8 + 2 + TOKENS * COLS * 4
@@ -41,12 +40,12 @@ def tile_geodesiclmheadv2_t_v_kernel(
 
     with ExitStack() as stack:
         keep = stack.enter_context(tc.tile_pool(name="keep", bufs=1))
-        x_pool = stack.enter_context(tc.tile_pool(name="x_pool", bufs=4))
+        x_pool = stack.enter_context(tc.tile_pool(name="x_pool", bufs=8))
         g_pool = stack.enter_context(tc.tile_pool(name="g_pool", bufs=3))
-        sq_pool = stack.enter_context(tc.tile_pool(name="sq_pool", bufs=3))
+        short_pool = stack.enter_context(tc.tile_pool(name="short_pool", bufs=4))
         long_pool = stack.enter_context(tc.tile_pool(name="long_pool", bufs=10))
         mx_pool = stack.enter_context(tc.tile_pool(name="mx_pool", bufs=3))
-        xt_psum = stack.enter_context(tc.psum_pool(name="xt_psum", bufs=X_BANKS))
+        xt_psum = stack.enter_context(tc.psum_pool(name="xt_psum", bufs=4))
         gt_psum = stack.enter_context(tc.psum_pool(name="gt_psum", bufs=2))
         acc_psum = stack.enter_context(tc.psum_pool(name="acc_psum", bufs=2))
         stack.enter_context(tc.manual_schedule())
@@ -55,32 +54,21 @@ def tile_geodesiclmheadv2_t_v_kernel(
         g_tiles = {}
         xt_tiles = {}
         gt_tiles = {}
+        u_tiles = {}
+        q_tiles = {}
         e_tiles = {}
         y_tiles = {}
         dx_tiles = {}
-        code_tiles = {}
         acc_tiles = {}
         o_tiles = {}
 
-        def load_x(pair):
-            if pair * X_PAIR >= TILES:
+        def load_x(i):
+            if i >= TILES:
                 return
-            first = pair * X_PAIR
-            c, n = divmod(first, CHUNK)
-            x_raw = x_pool.tile([P, X_PAIR, VOCAB], F32, name="x_raw")
-            nc.sync.dma_start(out=x_raw[:], in_=x_view[c, :, n : n + X_PAIR, :])
-            x_tiles[pair] = x_raw
-
-        def clamp(pair):
-            if pair * X_PAIR >= TILES:
-                return
-            flat = x_tiles[pair][:].rearrange("p n v -> p (n v)")
-            if pair % 2 == 0:
-                nc.vector.tensor_scalar(
-                    out=flat, in0=flat, scalar1=1.0, scalar2=-1.0, op0=ALU.max, op1=ALU.add
-                )
-            else:
-                nc.scalar.activation(out=flat, in_=flat, func=FUNC.Relu, bias=-1.0)
+            c, n = divmod(i, CHUNK)
+            x_raw = x_pool.tile([P, VOCAB], F32, name="x_raw")
+            nc.sync.dma_start(out=x_raw[:], in_=x_view[c, :, n, :])
+            x_tiles[i] = x_raw
 
         def load_g(quad):
             if quad * G_QUAD >= TILES:
@@ -90,6 +78,8 @@ def tile_geodesiclmheadv2_t_v_kernel(
             nc.sync.dma_start(out=g_raw[:], in_=g_view[c, :, n : n + G_QUAD, :])
             g_tiles[quad] = g_raw
 
+        for i in range(4):
+            load_x(i)
         ls_sb = keep.tile([P, 1], BF16, name="ls_sb")
         nc.sync.dma_start(out=ls_sb[:], in_=logit_scale.partition_broadcast(P))
         r_sb = keep.tile([P, PASSES, PACK], F32, name="r_sb")
@@ -97,41 +87,31 @@ def tile_geodesiclmheadv2_t_v_kernel(
         with nc.allow_non_contiguous_dma(reason="16-byte runs of two small vectors"):
             nc.sync.dma_start(out=r_sb[:], in_=r.rearrange("(g p j) -> p g j", p=P, j=PACK))
             nc.sync.dma_start(out=wt_sb[:], in_=w_time.rearrange("(g p j) -> p g j", p=P, j=PACK))
+        w_raw = keep.tile([P, PASSES, PACK, COLS - 1], BF16, name="w_raw")
+        nc.sync.dma_start(out=w_raw[:], in_=weight.rearrange("(g p j) w -> p g j w", p=P, j=PACK))
+        for i in range(4, 8):
+            load_x(i)
+        for quad in range(3):
+            load_g(quad)
 
         ident_f32 = keep.tile([P, P], F32, name="ident_f32")
         make_identity(nc, ident_f32[:])
         ident_bf16 = keep.tile([P, P], BF16, name="ident_bf16")
         make_identity(nc, ident_bf16[:])
 
-        load_x(0)
-        load_x(1)
-        w_raw = keep.tile([P, PASSES, PACK, COLS - 1], BF16, name="w_raw")
-        nc.sync.dma_start(
-            out=w_raw[:], in_=weight.rearrange("(g p j) w -> p g j w", p=P, j=PACK)
-        )
-        load_x(2)
-        load_x(3)
-        load_g(0)
-        load_g(1)
-        load_g(2)
-
         warm = keep.tile([P, 1], F32, name="warm")
         nc.vector.memset(warm[:], 1.0)
         nc.scalar.activation(out=warm[:], in_=warm[:], func=FUNC.Abs_reciprocal_sqrt)
 
-        c_sb = keep.tile([P, 1], F32, name="c_sb")
-        nc.vector.tensor_scalar(
-            out=c_sb[:], in0=ls_sb[:], scalar1=0.01, scalar2=2.5, op0=ALU.max, op1=ALU.min
-        )
-        nc.vector.tensor_scalar_mul(out=c_sb[:], in0=c_sb[:], scalar1=-2.0)
         neg_r = keep.tile([P, PASSES, PACK], F32, name="neg_r")
-        nc.vector.tensor_scalar_mul(out=neg_r[:], in0=r_sb[:], scalar1=-1.0)
+        nc.gpsimd.tensor_scalar(
+            out=neg_r[:], in0=r_sb[:], scalar1=-1.0, scalar2=0.0, op0=ALU.mult, op1=ALU.add
+        )
 
         w_grp = keep.tile([P, PASSES, COLS, PACK], BF16, name="w_grp", align_bytes=64)
         w_codes = keep.tile([P, PASSES, COLS], U32, name="w_codes", align_bytes=64)
         w_scales = keep.tile([P, PASSES, COLS], U8, name="w_scales", align_bytes=64)
-
-        def prepare_w(g):
+        for g in range(PASSES):
             nc.gpsimd.tensor_copy(out=w_grp[:, g, 0, :], in_=wt_sb[:, g, :])
             nc.gpsimd.tensor_tensor(
                 out=w_grp[:, g, 1:COLS, :],
@@ -147,48 +127,59 @@ def tile_geodesiclmheadv2_t_v_kernel(
                 in_=w_grp[:, g].rearrange("p w j -> p (w j)"),
             )
 
-        prepare_w(0)
-        prepare_w(1)
-
         def transpose_x(i):
             if i >= TILES:
                 return
-            x_raw = x_tiles[i // X_PAIR]
-            cols = x_raw[:, i % X_PAIR, :].rearrange("p (g c j) -> p g j c", g=PASSES, j=PACK)
+            cols = x_tiles.pop(i)[:].rearrange("p (g c j) -> p g j c", g=PASSES, j=PACK)
             for g in range(PASSES):
                 xt = xt_psum.tile([P, PACK, P], F32, name="xt")
                 for j in range(PACK):
                     nc.tensor.transpose(xt[:, j, :], cols[:, g, j, :], ident_f32[:])
                 xt_tiles[i, g] = xt
-            if i % X_PAIR == X_PAIR - 1:
-                load_x(i // X_PAIR + 4)
+            load_x(i + 8)
 
-        def front(i):
+        def scalar_front(i):
+            if i >= TILES:
+                return
+            u_sb = short_pool.tile([P, PASSES, P, PACK], F32, name="u_sb")
+            q_sb = short_pool.tile([P, PASSES, K_PASS], F32, name="q_sb")
             e_sb = long_pool.tile([P, PASSES, K_PASS], F32, name="e_sb")
-            y_sb = long_pool.tile([P, PASSES, K_PASS], F32, name="y_sb")
-            sq = sq_pool.tile([P, PASSES, K_PASS], F32, name="sq")
-            ut = [xt_tiles.pop((i, g))[:].rearrange("p j t -> p (j t)") for g in range(PASSES)]
-            for g in range(PASSES):
-                nc.scalar.activation(out=sq[:, g], in_=ut[g], func=FUNC.Square, bias=1.0)
             for g in range(PASSES):
                 nc.scalar.activation(
-                    out=e_sb[:, g], in_=sq[:, g], func=FUNC.Abs_reciprocal_sqrt, bias=-1.0
+                    out=u_sb[:, g], in_=xt_tiles.pop((i, g))[:].rearrange("p j t -> p t j"),
+                    func=FUNC.Relu, bias=-1.0,
+                )
+            transpose_x(i + 2)
+            for g in range(PASSES):
+                nc.scalar.activation(
+                    out=q_sb[:, g], in_=u_sb[:, g].rearrange("p t j -> p (t j)"),
+                    func=FUNC.Square, bias=1.0,
                 )
             for g in range(PASSES):
+                nc.scalar.activation(
+                    out=e_sb[:, g], in_=q_sb[:, g], func=FUNC.Abs_reciprocal_sqrt, bias=-1.0
+                )
+            u_tiles[i] = u_sb
+            q_tiles[i] = q_sb
+            e_tiles[i] = e_sb
+
+        def vector_front(i):
+            if i >= TILES:
+                return
+            u_sb = u_tiles.pop(i)
+            s_sb = q_tiles.pop(i)
+            y_sb = long_pool.tile([P, PASSES, K_PASS], F32, name="y_sb")
+            for g in range(PASSES):
                 nc.vector.scalar_tensor_tensor(
-                    out=sq[:, g], in0=sq[:, g], scalar=-1.0, in1=e_sb[:, g],
+                    out=s_sb[:, g], in0=s_sb[:, g], scalar=-1.0, in1=e_tiles[i][:, g],
                     op0=ALU.add, op1=ALU.mult,
                 )
             for g in range(PASSES):
                 nc.vector.scalar_tensor_tensor(
-                    out=y_sb[:, g], in0=ut[g], scalar=1.0, in1=sq[:, g],
-                    op0=ALU.add, op1=ALU.add,
+                    out=y_sb[:, g], in0=u_sb[:, g].rearrange("p t j -> p (t j)"), scalar=1.0,
+                    in1=s_sb[:, g], op0=ALU.add, op1=ALU.add,
                 )
-            e_tiles[i] = e_sb
             y_tiles[i] = y_sb
-            if (i + 3) % X_PAIR == 0:
-                clamp((i + 3) // X_PAIR)
-            transpose_x(i + 2)
 
         def log(i):
             flat = y_tiles[i][:].rearrange("p g k -> p (g k)")
@@ -221,7 +212,7 @@ def tile_geodesiclmheadv2_t_v_kernel(
             for g in range(PASSES):
                 nc.vector.scalar_tensor_tensor(
                     out=dx[:, g],
-                    in0=t_sb[:, g].rearrange("p (j t) -> p t j", j=PACK),
+                    in0=t_sb[:, g].rearrange("p (t j) -> p t j", j=PACK),
                     scalar=0.0,
                     in1=gt[:, g].rearrange("p j t -> p t j"),
                     op0=ALU.min, op1=ALU.mult,
@@ -256,20 +247,38 @@ def tile_geodesiclmheadv2_t_v_kernel(
         def drain(i):
             if i < 0:
                 return
+            if i % O_PAIR == 0:
+                o_tiles[i // O_PAIR] = mx_pool.tile([P, O_PAIR, COLS], F32, name="o_sb")
+            o_sb = o_tiles[i // O_PAIR]
             if i % 2 == 0:
-                o_tiles[i // 2] = mx_pool.tile([P, 2, COLS], F32, name="o_sb")
-            o_sb = o_tiles[i // 2]
-            nc.scalar.copy(out=o_sb[:, i % 2, :], in_=acc_tiles.pop(i)[:])
-            if i % 2 == 1:
-                c, n = divmod(i - 1, CHUNK)
-                nc.sync.dma_start(out=out_view[c, :, n : n + 2, :], in_=o_sb[:])
+                nc.vector.tensor_copy(out=o_sb[:, i % O_PAIR, :], in_=acc_tiles.pop(i)[:])
+            else:
+                nc.scalar.copy(out=o_sb[:, i % O_PAIR, :], in_=acc_tiles.pop(i)[:])
+            if i % O_PAIR == O_PAIR - 1:
+                c, n = divmod(i - (O_PAIR - 1), CHUNK)
+                nc.sync.dma_start(out=out_view[c, :, n : n + O_PAIR, :], in_=o_sb[:])
 
-        clamp(0)
+        def fronts(first):
+            for n in range(CHUNK):
+                if n + LEAD < CHUNK:
+                    scalar_front(first + n + LEAD)
+                vector_front(first + n)
+                late_back(first, n)
+
+        def late_back(first, n):
+            if first >= CHUNK and n % 2 == 1:
+                back(first - CHUNK + CHUNK // 2 + n // 2)
+
         transpose_x(0)
         transpose_x(1)
-        clamp(1)
-        for i in range(CHUNK):
-            front(i)
+        for n in range(LEAD):
+            scalar_front(n)
+        fronts(0)
+        c_sb = keep.tile([P, 1], F32, name="c_sb")
+        nc.vector.tensor_scalar(
+            out=c_sb[:], in0=ls_sb[:], scalar1=0.01, scalar2=2.5, op0=ALU.max, op1=ALU.min
+        )
+        nc.vector.tensor_scalar_mul(out=c_sb[:], in0=c_sb[:], scalar1=-2.0)
         quantise_w(0)
         quantise_w(1)
         transpose_g(0)
@@ -277,15 +286,12 @@ def tile_geodesiclmheadv2_t_v_kernel(
             first = c * CHUNK
             for n in range(CHUNK):
                 log(first + n)
-            for n in range(BACKS_DURING_LOGS):
+            for n in range(CHUNK // 2 - LEAD):
                 back(first + n)
-            late = BACKS_DURING_LOGS
-            for n in range(CHUNK):
-                if c + 1 < CHUNKS:
-                    front(first + CHUNK + n)
-                if n % 2 == 1 and n >= 3:
-                    back(first + late)
-                    late += 1
+            for n in range(LEAD):
+                scalar_front(first + CHUNK + n)
+                back(first + CHUNK // 2 - LEAD + n)
+            fronts(first + CHUNK)
         multiply(TILES - 1)
         drain(TILES - 2)
         drain(TILES - 1)

@@ -25,6 +25,7 @@ CHUNKS = TILES // CHUNK
 G_QUAD = 4
 O_PAIR = 2
 LEAD = 2
+EARLY = 5
 
 FLOPS = 2 * TOKENS * VOCAB * COLS
 BYTES = TOKENS * VOCAB * (4 + 2) + VOCAB * (COLS - 1) * 2 + VOCAB * 8 + 2 + TOKENS * COLS * 4
@@ -145,10 +146,13 @@ def tile_geodesiclmheadv2_t_v_kernel(
             q_sb = short_pool.tile([P, PASSES, K_PASS], F32, name="q_sb")
             e_sb = long_pool.tile([P, PASSES, K_PASS], F32, name="e_sb")
             for g in range(PASSES):
-                nc.scalar.activation(
-                    out=u_sb[:, g], in_=xt_tiles.pop((i, g))[:].rearrange("p j t -> p t j"),
-                    func=FUNC.Relu, bias=-1.0,
-                )
+                xt = xt_tiles.pop((i, g))[:].rearrange("p j t -> p t j")
+                if i < CHUNK and g == 1:
+                    nc.vector.tensor_scalar(
+                        out=u_sb[:, g], in0=xt, scalar1=1.0, scalar2=-1.0, op0=ALU.max, op1=ALU.add
+                    )
+                else:
+                    nc.scalar.activation(out=u_sb[:, g], in_=xt, func=FUNC.Relu, bias=-1.0)
             transpose_x(i + 2)
             for g in range(PASSES):
                 nc.scalar.activation(
@@ -250,7 +254,7 @@ def tile_geodesiclmheadv2_t_v_kernel(
             if i % O_PAIR == 0:
                 o_tiles[i // O_PAIR] = mx_pool.tile([P, O_PAIR, COLS], F32, name="o_sb")
             o_sb = o_tiles[i // O_PAIR]
-            if i % 2 == 0:
+            if i % 2 == 0 and i < TILES - CHUNK:
                 nc.vector.tensor_copy(out=o_sb[:, i % O_PAIR, :], in_=acc_tiles.pop(i)[:])
             else:
                 nc.scalar.copy(out=o_sb[:, i % O_PAIR, :], in_=acc_tiles.pop(i)[:])
@@ -266,8 +270,9 @@ def tile_geodesiclmheadv2_t_v_kernel(
                 late_back(first, n)
 
         def late_back(first, n):
-            if first >= CHUNK and n % 2 == 1:
-                back(first - CHUNK + CHUNK // 2 + n // 2)
+            from_end = (CHUNK - 1 - n) // 2
+            if first >= CHUNK and n % 2 == 1 and from_end < CHUNK - EARLY:
+                back(first - 1 - from_end)
 
         transpose_x(0)
         transpose_x(1)
@@ -286,11 +291,11 @@ def tile_geodesiclmheadv2_t_v_kernel(
             first = c * CHUNK
             for n in range(CHUNK):
                 log(first + n)
-            for n in range(CHUNK // 2 - LEAD):
+            for n in range(EARLY - LEAD):
                 back(first + n)
             for n in range(LEAD):
                 scalar_front(first + CHUNK + n)
-                back(first + CHUNK // 2 - LEAD + n)
+                back(first + EARLY - LEAD + n)
             fronts(first + CHUNK)
         multiply(TILES - 1)
         drain(TILES - 2)

@@ -97,8 +97,6 @@ def tile_geodesiclmheadv2_t_v_kernel(
 
         ident_f32 = keep.tile([P, P], F32, name="ident_f32")
         make_identity(nc, ident_f32[:])
-        ident_bf16 = keep.tile([P, P], BF16, name="ident_bf16")
-        make_identity(nc, ident_bf16[:])
 
         warm = keep.tile([P, 1], F32, name="warm")
         nc.vector.memset(warm[:], 1.0)
@@ -192,12 +190,12 @@ def tile_geodesiclmheadv2_t_v_kernel(
         def transpose_g(i):
             if i >= TILES:
                 return
-            g_raw = g_tiles[i // G_QUAD]
-            cols = g_raw[:, i % G_QUAD, :].rearrange("p (g c j) -> p g j c", g=PASSES, j=PACK)
-            gt = gt_psum.tile([P, PASSES, PACK, P], BF16, name="gt")
+            words = g_tiles[i // G_QUAD][:].bitcast(F32)
+            cols = words[:, i % G_QUAD, :].rearrange("p (g c h) -> p g h c", g=PASSES, h=PACK // 2)
+            gt = gt_psum.tile([P, PASSES, P, PACK // 2], F32, name="gt")
             for g in range(PASSES):
-                for j in range(PACK):
-                    nc.tensor.transpose(gt[:, g, j, :], cols[:, g, j, :], ident_bf16[:])
+                for h in range(PACK // 2):
+                    nc.tensor.transpose(gt[:, g, :, h], cols[:, g, h, :], ident_f32[:])
             gt_tiles[i] = gt
             if i % G_QUAD == G_QUAD - 1:
                 load_g(i // G_QUAD + 3)
@@ -212,13 +210,13 @@ def tile_geodesiclmheadv2_t_v_kernel(
                     op0=ALU.mult, op1=ALU.mult,
                 )
             gt = gt_tiles.pop(i)
-            dx = mx_pool.tile([P, PASSES, P, PACK], BF16, name="dx", align_bytes=64)
+            dx = mx_pool.tile([P, PASSES, K_PASS], BF16, name="dx", align_bytes=64)
             for g in range(PASSES):
                 nc.vector.scalar_tensor_tensor(
                     out=dx[:, g],
-                    in0=t_sb[:, g].rearrange("p (t j) -> p t j", j=PACK),
+                    in0=t_sb[:, g],
                     scalar=0.0,
-                    in1=gt[:, g].rearrange("p j t -> p t j"),
+                    in1=gt[:, g].rearrange("p t h -> p (t h)").bitcast(BF16),
                     op0=ALU.min, op1=ALU.mult,
                 )
             dx_tiles[i] = dx
@@ -233,7 +231,7 @@ def tile_geodesiclmheadv2_t_v_kernel(
             nc.vector.quantize_mx(
                 out=codes[:].rearrange("p g t -> p (g t)").bitcast(E5M2_X4),
                 scales=scales[:].rearrange("p g t -> p (g t)"),
-                in_=dx_tiles.pop(i)[:].rearrange("p g t j -> p (g t j)"),
+                in_=dx_tiles.pop(i)[:].rearrange("p g k -> p (g k)"),
             )
             acc = acc_psum.tile([P, COLS], F32, name="acc")
             for g in range(PASSES):

@@ -20,12 +20,15 @@ VOCAB = 1024
 COLS = 512
 PASSES = VOCAB // K_PASS
 TILES = TOKENS // P
-CHUNK = 8
-CHUNKS = TILES // CHUNK
+BLOCK = 8
+CHUNK_SIZES = (4, 8, 8, 8, 4)
+MAX_CHUNK = 8
 G_QUAD = 4
+Q_GROUP = 4
 O_PAIR = 2
-LEAD = 2
-EARLY = 5
+X_BUFS = 12
+Y_ON_VECTOR = 2
+DRAIN_FROM = 3
 
 FLOPS = 2 * TOKENS * VOCAB * COLS
 BYTES = TOKENS * VOCAB * (4 + 2) + VOCAB * (COLS - 1) * 2 + VOCAB * 8 + 2 + TOKENS * COLS * 4
@@ -35,38 +38,40 @@ def tile_geodesiclmheadv2_t_v_kernel(
     tc, hidden_states, weight, logit_scale, x, r, w_time, grad_out, out
 ):
     nc = tc.nc
-    x_view = x.flatten_outer_dims().rearrange("(c p n) v -> c p n v", p=P, n=CHUNK)
-    g_view = grad_out.flatten_outer_dims().rearrange("(c p n) v -> c p n v", p=P, n=CHUNK)
-    out_view = out.flatten_outer_dims().rearrange("(c p n) w -> c p n w", p=P, n=CHUNK)
+    x_view = x.flatten_outer_dims().rearrange("(c p n) v -> c p n v", p=P, n=BLOCK)
+    g_view = grad_out.flatten_outer_dims().rearrange("(c p n) v -> c p n v", p=P, n=BLOCK)
+    out_view = out.flatten_outer_dims().rearrange("(c p n) w -> c p n w", p=P, n=BLOCK)
 
     with ExitStack() as stack:
         keep = stack.enter_context(tc.tile_pool(name="keep", bufs=1))
-        x_pool = stack.enter_context(tc.tile_pool(name="x_pool", bufs=8))
+        x_pool = stack.enter_context(tc.tile_pool(name="x_pool", bufs=X_BUFS))
         g_pool = stack.enter_context(tc.tile_pool(name="g_pool", bufs=3))
-        short_pool = stack.enter_context(tc.tile_pool(name="short_pool", bufs=4))
-        long_pool = stack.enter_context(tc.tile_pool(name="long_pool", bufs=10))
-        mx_pool = stack.enter_context(tc.tile_pool(name="mx_pool", bufs=3))
-        xt_psum = stack.enter_context(tc.psum_pool(name="xt_psum", bufs=4))
-        gt_psum = stack.enter_context(tc.psum_pool(name="gt_psum", bufs=2))
-        acc_psum = stack.enter_context(tc.psum_pool(name="acc_psum", bufs=2))
+        q_pool = stack.enter_context(tc.tile_pool(name="q_pool", bufs=MAX_CHUNK + 1))
+        e_pool = stack.enter_context(tc.tile_pool(name="e_pool", bufs=MAX_CHUNK))
+        d_pool = stack.enter_context(tc.tile_pool(name="d_pool", bufs=4))
+        mx_pool = stack.enter_context(tc.tile_pool(name="mx_pool", bufs=2))
+        o_pool = stack.enter_context(tc.tile_pool(name="o_pool", bufs=3))
+        yt_psum = stack.enter_context(tc.psum_pool(name="yt_psum", bufs=2))
+        bank_psum = stack.enter_context(tc.psum_pool(name="bank_psum", bufs=6))
         stack.enter_context(tc.manual_schedule())
 
         x_tiles = {}
         g_tiles = {}
-        xt_tiles = {}
-        gt_tiles = {}
-        u_tiles = {}
         q_tiles = {}
         e_tiles = {}
-        y_tiles = {}
+        yt_tiles = {}
+        et_tiles = {}
+        gt_tiles = {}
+        d_tiles = {}
         dx_tiles = {}
+        code_tiles = {}
         acc_tiles = {}
         o_tiles = {}
 
         def load_x(i):
             if i >= TILES:
                 return
-            c, n = divmod(i, CHUNK)
+            c, n = divmod(i, BLOCK)
             x_raw = x_pool.tile([P, VOCAB], F32, name="x_raw")
             nc.sync.dma_start(out=x_raw[:], in_=x_view[c, :, n, :])
             x_tiles[i] = x_raw
@@ -74,8 +79,8 @@ def tile_geodesiclmheadv2_t_v_kernel(
         def load_g(quad):
             if quad * G_QUAD >= TILES:
                 return
-            c, n = divmod(quad * G_QUAD, CHUNK)
-            g_raw = g_pool.tile([P, G_QUAD, VOCAB], BF16, name="g_raw")
+            c, n = divmod(quad * G_QUAD, BLOCK)
+            g_raw = g_pool.tile([P, G_QUAD, VOCAB], BF16, name="g_raw", align_bytes=64)
             nc.sync.dma_start(out=g_raw[:], in_=g_view[c, :, n : n + G_QUAD, :])
             g_tiles[quad] = g_raw
 
@@ -88,12 +93,13 @@ def tile_geodesiclmheadv2_t_v_kernel(
         with nc.allow_non_contiguous_dma(reason="16-byte runs of two small vectors"):
             nc.sync.dma_start(out=r_sb[:], in_=r.rearrange("(g p j) -> p g j", p=P, j=PACK))
             nc.sync.dma_start(out=wt_sb[:], in_=w_time.rearrange("(g p j) -> p g j", p=P, j=PACK))
-        w_raw = keep.tile([P, PASSES, PACK, COLS - 1], BF16, name="w_raw")
-        nc.sync.dma_start(out=w_raw[:], in_=weight.rearrange("(g p j) w -> p g j w", p=P, j=PACK))
+        load_g(0)
         for i in range(4, 8):
             load_x(i)
-        for quad in range(3):
-            load_g(quad)
+        w_raw = g_pool.tile([P, PASSES, PACK, COLS - 1], BF16, name="w_raw", tag="g_raw", align_bytes=64)
+        nc.sync.dma_start(out=w_raw[:], in_=weight.rearrange("(g p j) w -> p g j w", p=P, j=PACK))
+        for i in range(8, X_BUFS):
+            load_x(i)
 
         ident_f32 = keep.tile([P, P], F32, name="ident_f32")
         make_identity(nc, ident_f32[:])
@@ -102,17 +108,23 @@ def tile_geodesiclmheadv2_t_v_kernel(
         nc.vector.memset(warm[:], 1.0)
         nc.scalar.activation(out=warm[:], in_=warm[:], func=FUNC.Abs_reciprocal_sqrt)
 
+        c_sb = keep.tile([P, 1], F32, name="c_sb")
+        nc.vector.tensor_scalar(
+            out=c_sb[:], in0=ls_sb[:], scalar1=0.01, scalar2=2.5, op0=ALU.max, op1=ALU.min
+        )
+        nc.vector.tensor_scalar_mul(out=c_sb[:], in0=c_sb[:], scalar1=-2.0)
+
         neg_r = keep.tile([P, PASSES, PACK], F32, name="neg_r")
         nc.gpsimd.tensor_scalar(
             out=neg_r[:], in0=r_sb[:], scalar1=-1.0, scalar2=0.0, op0=ALU.mult, op1=ALU.add
         )
 
-        w_grp = keep.tile([P, PASSES, COLS, PACK], BF16, name="w_grp", align_bytes=64)
+        w_grp = g_pool.tile([P, PASSES, COLS, PACK], BF16, name="w_grp", tag="g_raw", align_bytes=64)
         w_codes = keep.tile([P, PASSES, COLS], U32, name="w_codes", align_bytes=64)
         w_scales = keep.tile([P, PASSES, COLS], U8, name="w_scales", align_bytes=64)
-        for g in range(PASSES):
-            nc.gpsimd.tensor_copy(out=w_grp[:, g, 0, :], in_=wt_sb[:, g, :])
-            nc.gpsimd.tensor_tensor(
+        def make_w(g):
+            nc.vector.tensor_copy(out=w_grp[:, g, 0, :], in_=wt_sb[:, g, :])
+            nc.vector.tensor_tensor(
                 out=w_grp[:, g, 1:COLS, :],
                 in0=w_raw[:, g].rearrange("p j w -> p w j"),
                 in1=neg_r[:, g, :].unsqueeze(1).to_broadcast([P, COLS - 1, PACK]),
@@ -126,119 +138,116 @@ def tile_geodesiclmheadv2_t_v_kernel(
                 in_=w_grp[:, g].rearrange("p w j -> p (w j)"),
             )
 
-        def transpose_x(i):
-            if i >= TILES:
-                return
-            cols = x_tiles.pop(i)[:].rearrange("p (g c j) -> p g j c", g=PASSES, j=PACK)
-            for g in range(PASSES):
-                xt = xt_psum.tile([P, PACK, P], F32, name="xt")
-                for j in range(PACK):
-                    nc.tensor.transpose(xt[:, j, :], cols[:, g, j, :], ident_f32[:])
-                xt_tiles[i, g] = xt
-            load_x(i + 8)
+        def by_word(x_raw):
+            return x_raw[:].rearrange("p (g c j) -> p g c j", g=PASSES, j=PACK)
 
-        def scalar_front(i):
+        def square(i):
             if i >= TILES:
                 return
-            u_sb = short_pool.tile([P, PASSES, P, PACK], F32, name="u_sb")
-            q_sb = short_pool.tile([P, PASSES, K_PASS], F32, name="q_sb")
-            e_sb = long_pool.tile([P, PASSES, K_PASS], F32, name="e_sb")
-            for g in range(PASSES):
-                xt = xt_tiles.pop((i, g))[:].rearrange("p j t -> p t j")
-                if i < CHUNK and g == 1:
-                    nc.vector.tensor_scalar(
-                        out=u_sb[:, g], in0=xt, scalar1=1.0, scalar2=-1.0, op0=ALU.max, op1=ALU.add
-                    )
-                else:
-                    nc.scalar.activation(out=u_sb[:, g], in_=xt, func=FUNC.Relu, bias=-1.0)
-            transpose_x(i + 2)
-            for g in range(PASSES):
-                nc.scalar.activation(
-                    out=q_sb[:, g], in_=u_sb[:, g].rearrange("p t j -> p (t j)"),
-                    func=FUNC.Square, bias=1.0,
-                )
-            for g in range(PASSES):
-                nc.scalar.activation(
-                    out=e_sb[:, g], in_=q_sb[:, g], func=FUNC.Abs_reciprocal_sqrt, bias=-1.0
-                )
-            u_tiles[i] = u_sb
+            q_sb = q_pool.tile([P, PASSES, P, PACK], F32, name="q_sb")
+            nc.scalar.activation(out=q_sb[:], in_=by_word(x_tiles[i]), func=FUNC.Square)
             q_tiles[i] = q_sb
+
+        def inverse_root(i):
+            if i >= TILES:
+                return
+            e_sb = e_pool.tile([P, PASSES, P, PACK], F32, name="e_sb")
+            nc.scalar.activation(
+                out=e_sb[:], in_=q_tiles[i][:], func=FUNC.Abs_reciprocal_sqrt, bias=-1.0
+            )
             e_tiles[i] = e_sb
 
-        def vector_front(i):
+        def root(i):
             if i >= TILES:
                 return
-            u_sb = u_tiles.pop(i)
-            s_sb = q_tiles.pop(i)
-            y_sb = long_pool.tile([P, PASSES, K_PASS], F32, name="y_sb")
-            for g in range(PASSES):
-                nc.vector.scalar_tensor_tensor(
-                    out=s_sb[:, g], in0=s_sb[:, g], scalar=-1.0, in1=e_tiles[i][:, g],
-                    op0=ALU.add, op1=ALU.mult,
-                )
-            for g in range(PASSES):
-                nc.vector.scalar_tensor_tensor(
-                    out=y_sb[:, g], in0=u_sb[:, g].rearrange("p t j -> p (t j)"), scalar=1.0,
-                    in1=s_sb[:, g], op0=ALU.add, op1=ALU.add,
-                )
-            y_tiles[i] = y_sb
+            nc.vector.scalar_tensor_tensor(
+                out=q_tiles[i][:], in0=q_tiles[i][:], scalar=-1.0, in1=e_tiles[i][:],
+                op0=ALU.add, op1=ALU.mult,
+            )
 
-        def log(i):
-            flat = y_tiles[i][:].rearrange("p g k -> p (g k)")
-            nc.scalar.activation(out=flat, in_=flat, func=FUNC.Ln)
+        def add_x(i, on_vector):
+            x_raw = x_tiles.pop(i)
+            if on_vector:
+                nc.vector.tensor_tensor(
+                    out=q_tiles[i][:], in0=by_word(x_raw), in1=q_tiles[i][:], op=ALU.add
+                )
+            else:
+                for g in range(PASSES):
+                    nc.gpsimd.tensor_tensor(
+                        out=q_tiles[i][:, g], in0=by_word(x_raw)[:, g], in1=q_tiles[i][:, g], op=ALU.add
+                    )
+            load_x(i + X_BUFS)
+
+        def transpose_y(i, g):
+            yt = yt_psum.tile([P, PACK, P], F32, name="yt")
+            for j in range(PACK):
+                nc.tensor.transpose(yt[:, j, :], q_tiles[i][:, g, :, j], ident_f32[:])
+            yt_tiles[i, g] = yt
+
+        def transpose_e(i, g):
+            et = bank_psum.tile([P, PACK, P], F32, name="et", tag="bank")
+            for j in range(PACK):
+                nc.tensor.transpose(et[:, j, :], e_tiles[i][:, g, :, j], ident_f32[:])
+            et_tiles[i, g] = et
 
         def transpose_g(i):
-            if i >= TILES:
-                return
             words = g_tiles[i // G_QUAD][:].bitcast(F32)
             cols = words[:, i % G_QUAD, :].rearrange("p (g c h) -> p g h c", g=PASSES, h=PACK // 2)
-            gt = gt_psum.tile([P, PASSES, P, PACK // 2], F32, name="gt")
+            gt = bank_psum.tile([P, PASSES, P, PACK // 2], F32, name="gt", tag="bank")
             for g in range(PASSES):
                 for h in range(PACK // 2):
                     nc.tensor.transpose(gt[:, g, :, h], cols[:, g, h, :], ident_f32[:])
             gt_tiles[i] = gt
-            if i % G_QUAD == G_QUAD - 1:
+            if i % G_QUAD == G_QUAD - 1 and i > G_QUAD:
                 load_g(i // G_QUAD + 3)
 
-        def back(i):
-            transpose_g(i + 1)
-            t_sb = y_tiles.pop(i)
-            e_sb = e_tiles.pop(i)
-            for g in range(PASSES):
-                nc.vector.scalar_tensor_tensor(
-                    out=t_sb[:, g], in0=t_sb[:, g], scalar=c_sb[:, 0:1], in1=e_sb[:, g],
-                    op0=ALU.mult, op1=ALU.mult,
-                )
-            gt = gt_tiles.pop(i)
-            dx = mx_pool.tile([P, PASSES, K_PASS], BF16, name="dx", align_bytes=64)
-            for g in range(PASSES):
-                nc.vector.scalar_tensor_tensor(
-                    out=dx[:, g],
-                    in0=t_sb[:, g],
-                    scalar=0.0,
-                    in1=gt[:, g].rearrange("p t h -> p (t h)").bitcast(BF16),
-                    op0=ALU.min, op1=ALU.mult,
-                )
-            dx_tiles[i] = dx
-            multiply(i - 1)
-            drain(i - 2)
+        def log(i, g):
+            if g == 0:
+                d_tiles[i] = d_pool.tile([P, PASSES, P, PACK], F32, name="d_sb")
+            nc.scalar.activation(
+                out=d_tiles[i][:, g], in_=yt_tiles.pop((i, g))[:].rearrange("p j t -> p t j"), func=FUNC.Ln
+            )
+
+        def times_e(i, g):
+            nc.vector.scalar_tensor_tensor(
+                out=d_tiles[i][:, g], in0=d_tiles[i][:, g], scalar=c_sb[:, 0:1],
+                in1=et_tiles.pop((i, g))[:].rearrange("p j t -> p t j"),
+                op0=ALU.mult, op1=ALU.mult,
+            )
+
+        def times_g(i):
+            group, k = divmod(i, Q_GROUP)
+            if k == 0:
+                dx_tiles[group] = mx_pool.tile([P, Q_GROUP, VOCAB], BF16, name="dx", align_bytes=64)
+            nc.vector.scalar_tensor_tensor(
+                out=dx_tiles[group][:, k, :],
+                in0=d_tiles.pop(i)[:].rearrange("p g t j -> p (g t j)"),
+                scalar=0.0,
+                in1=gt_tiles.pop(i)[:].rearrange("p g t h -> p (g t h)").bitcast(BF16),
+                op0=ALU.min, op1=ALU.mult,
+            )
+
+        def quantise(group, k, count):
+            if k == 0:
+                codes = mx_pool.tile([P, Q_GROUP, PASSES, P], U32, name="codes", align_bytes=64)
+                scales = mx_pool.tile([P, Q_GROUP, PASSES, P], U8, name="scales", align_bytes=64)
+                code_tiles[group] = (codes, scales)
+            codes, scales = code_tiles[group]
+            nc.vector.quantize_mx(
+                out=codes[:, k : k + count].rearrange("p k g t -> p (k g t)").bitcast(E5M2_X4),
+                scales=scales[:, k : k + count].rearrange("p k g t -> p (k g t)"),
+                in_=dx_tiles[group][:, k : k + count, :].rearrange("p k v -> p (k v)"),
+            )
 
         def multiply(i):
-            if i < 0:
-                return
-            codes = mx_pool.tile([P, PASSES, P], U32, name="codes", align_bytes=64)
-            scales = mx_pool.tile([P, PASSES, P], U8, name="scales", align_bytes=64)
-            nc.vector.quantize_mx(
-                out=codes[:].rearrange("p g t -> p (g t)").bitcast(E5M2_X4),
-                scales=scales[:].rearrange("p g t -> p (g t)"),
-                in_=dx_tiles.pop(i)[:].rearrange("p g k -> p (g k)"),
-            )
-            acc = acc_psum.tile([P, COLS], F32, name="acc")
+            codes, scales = code_tiles[i // Q_GROUP]
+            k = i % Q_GROUP
+            acc = bank_psum.tile([P, COLS], F32, name="acc", tag="bank")
             for g in range(PASSES):
                 nc.tensor.matmul_mx(
                     out=acc[:],
-                    lhsT=codes[:, g, :].bitcast(E5M2_X4),
-                    lhsT_scale=scales[:, g, :],
+                    lhsT=codes[:, k, g, :].bitcast(E5M2_X4),
+                    lhsT_scale=scales[:, k, g, :],
                     rhs=w_codes[:, g, :].bitcast(E4M3_X4),
                     rhs_scale=w_scales[:, g, :],
                     start=(g == 0),
@@ -246,55 +255,113 @@ def tile_geodesiclmheadv2_t_v_kernel(
                 )
             acc_tiles[i] = acc
 
-        def drain(i):
-            if i < 0:
-                return
+        def drain(i, on_scalar):
             if i % O_PAIR == 0:
-                o_tiles[i // O_PAIR] = mx_pool.tile([P, O_PAIR, COLS], F32, name="o_sb")
+                o_tiles[i // O_PAIR] = o_pool.tile([P, O_PAIR, COLS], F32, name="o_sb")
             o_sb = o_tiles[i // O_PAIR]
-            if i % 2 == 0 and i < TILES - CHUNK:
-                nc.vector.tensor_copy(out=o_sb[:, i % O_PAIR, :], in_=acc_tiles.pop(i)[:])
-            else:
+            if on_scalar:
                 nc.scalar.copy(out=o_sb[:, i % O_PAIR, :], in_=acc_tiles.pop(i)[:])
+            else:
+                nc.vector.tensor_copy(out=o_sb[:, i % O_PAIR, :], in_=acc_tiles.pop(i)[:])
             if i % O_PAIR == O_PAIR - 1:
-                c, n = divmod(i - (O_PAIR - 1), CHUNK)
+                c, n = divmod(i - (O_PAIR - 1), BLOCK)
                 nc.sync.dma_start(out=out_view[c, :, n : n + O_PAIR, :], in_=o_sb[:])
 
-        def fronts(first):
-            for n in range(CHUNK):
-                if n + LEAD < CHUNK:
-                    scalar_front(first + n + LEAD)
-                vector_front(first + n)
-                late_back(first, n)
+        def first_half(first, size, in_step):
+            order = list(range(Y_ON_VECTOR)) + list(range(Y_ON_VECTOR + 1, size)) + [Y_ON_VECTOR]
+            waiting = []
+            for k, n in enumerate(order):
+                inverse_root(first + n)
+                in_step(k)
+                root(first + n)
+                if waiting:
+                    add_x(first + waiting.pop(0), True)
+                if n < Y_ON_VECTOR:
+                    waiting.append(n)
+            for n in range(Y_ON_VECTOR, size):
+                add_x(first + n, False)
 
-        def late_back(first, n):
-            from_end = (CHUNK - 1 - n) // 2
-            if first >= CHUNK and n % 2 == 1 and from_end < CHUNK - EARLY:
-                back(first - 1 - from_end)
+        def second_half(first, size, squares, after_product):
+            per_step = -(-len(squares) // size)
+            transpose_y(first, 0)
+            transpose_y(first, 1)
+            for n in range(size):
+                i = first + n
+                log(i, 0)
+                if n + 1 < size:
+                    transpose_y(i + 1, 0)
+                transpose_e(i, 0)
+                log(i, 1)
+                if n + 1 < size:
+                    transpose_y(i + 1, 1)
+                transpose_e(i, 1)
+                transpose_g(i)
+                for j in squares[n * per_step : (n + 1) * per_step]:
+                    square(j)
+                times_e(i, 0)
+                times_e(i, 1)
+                if n > 0:
+                    times_g(i - 1)
+                    after_product(i - 1)
+            times_g(first + size - 1)
+            after_product(first + size - 1)
 
-        transpose_x(0)
-        transpose_x(1)
-        for n in range(LEAD):
-            scalar_front(n)
-        fronts(0)
-        c_sb = keep.tile([P, 1], F32, name="c_sb")
-        nc.vector.tensor_scalar(
-            out=c_sb[:], in0=ls_sb[:], scalar1=0.01, scalar2=2.5, op0=ALU.max, op1=ALU.min
-        )
-        nc.vector.tensor_scalar_mul(out=c_sb[:], in0=c_sb[:], scalar1=-2.0)
-        quantise_w(0)
-        quantise_w(1)
-        transpose_g(0)
-        for c in range(CHUNKS):
-            first = c * CHUNK
-            for n in range(CHUNK):
-                log(first + n)
-            for n in range(EARLY - LEAD):
-                back(first + n)
-            for n in range(LEAD):
-                scalar_front(first + CHUNK + n)
-                back(first + EARLY - LEAD + n)
-            fronts(first + CHUNK)
-        multiply(TILES - 1)
-        drain(TILES - 2)
-        drain(TILES - 1)
+        bounds = [sum(CHUNK_SIZES[:k]) for k in range(len(CHUNK_SIZES) + 1)]
+
+        first_order = list(range(Y_ON_VECTOR)) + list(range(Y_ON_VECTOR + 1, CHUNK_SIZES[0])) + [Y_ON_VECTOR]
+
+        def squares_ahead(k):
+            if k + 1 < CHUNK_SIZES[0]:
+                square(first_order[k + 1])
+
+        square(first_order[0])
+        first_half(0, CHUNK_SIZES[0], squares_ahead)
+
+        for c, size in enumerate(CHUNK_SIZES):
+            first = bounds[c]
+            last_chunk = c + 1 == len(CHUNK_SIZES)
+            after = 0 if last_chunk else CHUNK_SIZES[c + 1]
+            def w_beside(i):
+                if i == size - 2:
+                    for g in range(PASSES):
+                        make_w(g)
+                if i == size - 1:
+                    for g in range(PASSES):
+                        quantise_w(g)
+                    for quad in range(1, 4):
+                        load_g(quad)
+
+            def finish(i):
+                quantise(i // Q_GROUP, i % Q_GROUP, 1)
+                if i > first:
+                    multiply(i - 1)
+                if i > first + 1:
+                    drain(i - 2, True)
+
+            def nothing(i):
+                return
+
+            second_half(
+                first, size, list(range(first + size, first + size + after)),
+                w_beside if c == 0 else finish if last_chunk else nothing,
+            )
+            if last_chunk:
+                multiply(first + size - 1)
+                drain(first + size - 2, True)
+                drain(first + size - 1, True)
+            else:
+                for group in range(first // Q_GROUP, (first + size) // Q_GROUP):
+                    quantise(group, 0, Q_GROUP)
+                for n in range(size):
+                    multiply(first + n)
+                on_scalar = list(range(first, first + size * 3 // 4))
+
+                def scalar_drains(k):
+                    if k >= DRAIN_FROM and on_scalar:
+                        drain(on_scalar.pop(0), True)
+
+                first_half(first + size, after, scalar_drains)
+                while on_scalar:
+                    drain(on_scalar.pop(0), True)
+                for i in range(first + size * 3 // 4, first + size):
+                    drain(i, False)

@@ -27,6 +27,7 @@ G_QUAD = 4
 Q_GROUP = 4
 O_PAIR = 2
 X_BUFS = 12
+E_AHEAD = 2
 Y_ON_VECTOR = 2
 DRAIN_FROM = 3
 
@@ -107,12 +108,6 @@ def tile_geodesiclmheadv2_t_v_kernel(
         warm = keep.tile([P, 1], F32, name="warm")
         nc.vector.memset(warm[:], 1.0)
         nc.scalar.activation(out=warm[:], in_=warm[:], func=FUNC.Abs_reciprocal_sqrt)
-
-        c_sb = keep.tile([P, 1], F32, name="c_sb")
-        nc.vector.tensor_scalar(
-            out=c_sb[:], in0=ls_sb[:], scalar1=0.01, scalar2=2.5, op0=ALU.max, op1=ALU.min
-        )
-        nc.vector.tensor_scalar_mul(out=c_sb[:], in0=c_sb[:], scalar1=-2.0)
 
         neg_r = keep.tile([P, PASSES, PACK], F32, name="neg_r")
         nc.gpsimd.tensor_scalar(
@@ -283,19 +278,21 @@ def tile_geodesiclmheadv2_t_v_kernel(
 
         def second_half(first, size, squares, after_product):
             per_step = -(-len(squares) // size)
-            transpose_y(first, 0)
-            transpose_y(first, 1)
+            for g in range(PASSES):
+                transpose_y(first, g)
+            for i in range(first, first + E_AHEAD):
+                for g in range(PASSES):
+                    transpose_e(i, g)
             for n in range(size):
                 i = first + n
-                log(i, 0)
-                if n + 1 < size:
-                    transpose_y(i + 1, 0)
-                transpose_e(i, 0)
-                log(i, 1)
-                if n + 1 < size:
-                    transpose_y(i + 1, 1)
-                transpose_e(i, 1)
+                for g in range(PASSES):
+                    log(i, g)
+                    if n + 1 < size:
+                        transpose_y(i + 1, g)
                 transpose_g(i)
+                if n + E_AHEAD < size:
+                    for g in range(PASSES):
+                        transpose_e(i + E_AHEAD, g)
                 for j in squares[n * per_step : (n + 1) * per_step]:
                     square(j)
                 times_e(i, 0)
@@ -316,16 +313,20 @@ def tile_geodesiclmheadv2_t_v_kernel(
 
         square(first_order[0])
         first_half(0, CHUNK_SIZES[0], squares_ahead)
+        c_sb = keep.tile([P, 1], F32, name="c_sb")
+        nc.vector.tensor_scalar(
+            out=c_sb[:], in0=ls_sb[:], scalar1=0.01, scalar2=2.5, op0=ALU.max, op1=ALU.min
+        )
+        nc.vector.tensor_scalar_mul(out=c_sb[:], in0=c_sb[:], scalar1=-2.0)
 
         for c, size in enumerate(CHUNK_SIZES):
             first = bounds[c]
             last_chunk = c + 1 == len(CHUNK_SIZES)
             after = 0 if last_chunk else CHUNK_SIZES[c + 1]
             def w_beside(i):
-                if i == size - 2:
-                    for g in range(PASSES):
-                        make_w(g)
-                if i == size - 1:
+                if i < PASSES:
+                    make_w(i)
+                if i == PASSES:
                     for g in range(PASSES):
                         quantise_w(g)
                     for quad in range(1, 4):

@@ -27,6 +27,7 @@ G_QUAD = 4
 Q_GROUP = 4
 O_PAIR = 2
 X_BUFS = 12
+EARLY_Q = 0
 E_AHEAD = 2
 Y_ON_VECTOR = 2
 DRAIN_FROM = 3
@@ -118,8 +119,8 @@ def tile_geodesiclmheadv2_t_v_kernel(
         w_codes = keep.tile([P, PASSES, COLS], U32, name="w_codes", align_bytes=64)
         w_scales = keep.tile([P, PASSES, COLS], U8, name="w_scales", align_bytes=64)
         def make_w(g):
-            nc.vector.tensor_copy(out=w_grp[:, g, 0, :], in_=wt_sb[:, g, :])
-            nc.vector.tensor_tensor(
+            nc.gpsimd.tensor_copy(out=w_grp[:, g, 0, :], in_=wt_sb[:, g, :])
+            nc.gpsimd.tensor_tensor(
                 out=w_grp[:, g, 1:COLS, :],
                 in0=w_raw[:, g].rearrange("p j w -> p w j"),
                 in1=neg_r[:, g, :].unsqueeze(1).to_broadcast([P, COLS - 1, PACK]),
@@ -293,7 +294,7 @@ def tile_geodesiclmheadv2_t_v_kernel(
                 if n + E_AHEAD < size:
                     for g in range(PASSES):
                         transpose_e(i + E_AHEAD, g)
-                for j in squares[n * per_step : (n + 1) * per_step]:
+                for j in squares[(n + 1) * per_step if n else 0 : (n + 2) * per_step]:
                     square(j)
                 times_e(i, 0)
                 times_e(i, 1)
@@ -313,6 +314,8 @@ def tile_geodesiclmheadv2_t_v_kernel(
 
         square(first_order[0])
         first_half(0, CHUNK_SIZES[0], squares_ahead)
+        for g in range(PASSES):
+            make_w(g)
         c_sb = keep.tile([P, 1], F32, name="c_sb")
         nc.vector.tensor_scalar(
             out=c_sb[:], in0=ls_sb[:], scalar1=0.01, scalar2=2.5, op0=ALU.max, op1=ALU.min
@@ -324,34 +327,37 @@ def tile_geodesiclmheadv2_t_v_kernel(
             last_chunk = c + 1 == len(CHUNK_SIZES)
             after = 0 if last_chunk else CHUNK_SIZES[c + 1]
             def w_beside(i):
-                if i < PASSES:
-                    make_w(i)
-                if i == PASSES:
+                if i == size - 1:
                     for g in range(PASSES):
                         quantise_w(g)
                     for quad in range(1, 4):
                         load_g(quad)
 
             def finish(i):
-                quantise(i // Q_GROUP, i % Q_GROUP, 1)
                 if i > first:
-                    multiply(i - 1)
+                    quantise((i - 1) // Q_GROUP, (i - 1) % Q_GROUP, 1)
                 if i > first + 1:
-                    drain(i - 2, True)
+                    multiply(i - 2)
+                if i > first + 2:
+                    drain(i - 3, True)
 
-            def nothing(i):
-                return
+            def early_groups(i):
+                if i == first + Q_GROUP + EARLY_Q:
+                    quantise(first // Q_GROUP, 0, Q_GROUP)
 
             second_half(
                 first, size, list(range(first + size, first + size + after)),
-                w_beside if c == 0 else finish if last_chunk else nothing,
+                w_beside if c == 0 else finish if last_chunk else early_groups,
             )
             if last_chunk:
-                multiply(first + size - 1)
-                drain(first + size - 2, True)
-                drain(first + size - 1, True)
+                quantise((TILES - 1) // Q_GROUP, (TILES - 1) % Q_GROUP, 1)
+                multiply(TILES - 2)
+                drain(TILES - 3, True)
+                multiply(TILES - 1)
+                drain(TILES - 2, True)
+                drain(TILES - 1, True)
             else:
-                for group in range(first // Q_GROUP, (first + size) // Q_GROUP):
+                for group in range(first // Q_GROUP + (1 if c else 0), (first + size) // Q_GROUP):
                     quantise(group, 0, Q_GROUP)
                 for n in range(size):
                     multiply(first + n)

@@ -29,7 +29,7 @@ O_PAIR = 2
 X_BUFS = 12
 EARLY_Q = 0
 E_AHEAD = 2
-Y_ON_VECTOR = 2
+Y_ON_VECTOR = 3
 DRAIN_FROM = 3
 
 FLOPS = 2 * TOKENS * VOCAB * COLS

@@ -168,10 +168,7 @@ def tile_geodesiclmheadv2_t_v_kernel(
                     out=q_tiles[i][:], in0=by_word(x_raw), in1=q_tiles[i][:], op=ALU.add
                 )
             else:
-                for g in range(PASSES):
-                    nc.gpsimd.tensor_tensor(
-                        out=q_tiles[i][:, g], in0=by_word(x_raw)[:, g], in1=q_tiles[i][:, g], op=ALU.add
-                    )
+                nc.gpsimd.tensor_tensor(out=q_tiles[i][:], in0=by_word(x_raw), in1=q_tiles[i][:], op=ALU.add)
             load_x(i + X_BUFS)
 
         def transpose_y(i, g):

@@ -144,6 +144,11 @@ def tile_geodesiclmheadv2_t_v_kernel(
             nc.scalar.activation(out=q_sb[:], in_=by_word(x_tiles[i]), func=FUNC.Square)
             q_tiles[i] = q_sb
 
+        def square_on_vector(i):
+            q_sb = q_pool.tile([P, PASSES, P, PACK], F32, name="q_sb")
+            nc.vector.tensor_tensor(out=q_sb[:], in0=by_word(x_tiles[i]), in1=by_word(x_tiles[i]), op=ALU.mult)
+            q_tiles[i] = q_sb
+
         def inverse_root(i):
             if i >= TILES:
                 return
@@ -256,9 +261,11 @@ def tile_geodesiclmheadv2_t_v_kernel(
                 nc.scalar.copy(out=o_sb[:, i % O_PAIR, :], in_=acc_tiles.pop(i)[:])
             else:
                 nc.vector.tensor_copy(out=o_sb[:, i % O_PAIR, :], in_=acc_tiles.pop(i)[:])
-            if i % O_PAIR == O_PAIR - 1:
-                c, n = divmod(i - (O_PAIR - 1), BLOCK)
-                nc.sync.dma_start(out=out_view[c, :, n : n + O_PAIR, :], in_=o_sb[:])
+            c, n = divmod(i, BLOCK)
+            if i >= TILES - O_PAIR:
+                nc.sync.dma_start(out=out_view[c, :, n, :], in_=o_sb[:, i % O_PAIR, :])
+            elif i % O_PAIR == O_PAIR - 1:
+                nc.sync.dma_start(out=out_view[c, :, n - (O_PAIR - 1) : n + 1, :], in_=o_sb[:])
 
         def first_half(first, size, in_step):
             order = list(range(Y_ON_VECTOR)) + list(range(Y_ON_VECTOR + 1, size)) + [Y_ON_VECTOR]
@@ -307,7 +314,10 @@ def tile_geodesiclmheadv2_t_v_kernel(
 
         def squares_ahead(k):
             if k + 1 < CHUNK_SIZES[0]:
-                square(first_order[k + 1])
+                if k == 0:
+                    square_on_vector(first_order[k + 1])
+                else:
+                    square(first_order[k + 1])
 
         square(first_order[0])
         first_half(0, CHUNK_SIZES[0], squares_ahead)

@@ -29,7 +29,8 @@ O_PAIR = 2
 X_BUFS = 12
 EARLY_Q = 0
 E_AHEAD = 2
-Y_ON_VECTOR = 3
+Y_ON_VECTOR = (3, 3, 3, 3, 2)
+LATE_SQUARES = 1
 DRAIN_FROM = 3
 
 FLOPS = 2 * TOKENS * VOCAB * COLS
@@ -267,18 +268,24 @@ def tile_geodesiclmheadv2_t_v_kernel(
             elif i % O_PAIR == O_PAIR - 1:
                 nc.sync.dma_start(out=out_view[c, :, n - (O_PAIR - 1) : n + 1, :], in_=o_sb[:])
 
-        def first_half(first, size, in_step):
-            order = list(range(Y_ON_VECTOR)) + list(range(Y_ON_VECTOR + 1, size)) + [Y_ON_VECTOR]
+        def chunk_order(c):
+            on_vector = Y_ON_VECTOR[c]
+            return list(range(on_vector)) + list(range(on_vector + 1, CHUNK_SIZES[c])) + [on_vector]
+
+        def first_half(c, in_step):
+            first, size = bounds[c], CHUNK_SIZES[c]
             waiting = []
-            for k, n in enumerate(order):
+            for k, n in enumerate(chunk_order(c)):
+                if first + n not in q_tiles:
+                    square(first + n)
                 inverse_root(first + n)
                 in_step(k)
                 root(first + n)
                 if waiting:
                     add_x(first + waiting.pop(0), True)
-                if n < Y_ON_VECTOR:
+                if n < Y_ON_VECTOR[c]:
                     waiting.append(n)
-            for n in range(Y_ON_VECTOR, size):
+            for n in range(Y_ON_VECTOR[c], size):
                 add_x(first + n, False)
 
         def second_half(first, size, squares, after_product):
@@ -310,7 +317,7 @@ def tile_geodesiclmheadv2_t_v_kernel(
 
         bounds = [sum(CHUNK_SIZES[:k]) for k in range(len(CHUNK_SIZES) + 1)]
 
-        first_order = list(range(Y_ON_VECTOR)) + list(range(Y_ON_VECTOR + 1, CHUNK_SIZES[0])) + [Y_ON_VECTOR]
+        first_order = chunk_order(0)
 
         def squares_ahead(k):
             if k + 1 < CHUNK_SIZES[0]:
@@ -320,7 +327,7 @@ def tile_geodesiclmheadv2_t_v_kernel(
                     square(first_order[k + 1])
 
         square(first_order[0])
-        first_half(0, CHUNK_SIZES[0], squares_ahead)
+        first_half(0, squares_ahead)
         for g in range(PASSES):
             make_w(g)
         c_sb = keep.tile([P, 1], F32, name="c_sb")
@@ -352,8 +359,11 @@ def tile_geodesiclmheadv2_t_v_kernel(
                 if i == first + Q_GROUP + EARLY_Q:
                     quantise(first // Q_GROUP, 0, Q_GROUP)
 
+            ahead = [] if last_chunk else [first + size + n for n in chunk_order(c + 1)]
+            if c == 0:
+                ahead = ahead[: len(ahead) - LATE_SQUARES]
             second_half(
-                first, size, list(range(first + size, first + size + after)),
+                first, size, sorted(ahead),
                 w_beside if c == 0 else finish if last_chunk else early_groups,
             )
             if last_chunk:
@@ -374,7 +384,7 @@ def tile_geodesiclmheadv2_t_v_kernel(
                     if k >= DRAIN_FROM and on_scalar:
                         drain(on_scalar.pop(0), True)
 
-                first_half(first + size, after, scalar_drains)
+                first_half(c + 1, scalar_drains)
                 while on_scalar:
                     drain(on_scalar.pop(0), True)
                 for i in range(first + size * 3 // 4, first + size):

from contextlib import ExitStack

import concourse.mybir as mybir
from concourse.masks import make_identity

F32 = mybir.dt.float32
BF16 = mybir.dt.bfloat16
U32 = mybir.dt.uint32
U8 = mybir.dt.uint8
E5M2_X4 = mybir.dt.float8_e5m2_x4
E4M3_X4 = mybir.dt.float8_e4m3fn_x4
ALU = mybir.AluOpType
FUNC = mybir.ActivationFunctionType

P = 128
PACK = 4
K_PASS = P * PACK
TOKENS = 4096
VOCAB = 1024
COLS = 512
PASSES = VOCAB // K_PASS
TILES = TOKENS // P
BLOCK = 8
CHUNK_SIZES = (4, 8, 8, 8, 4)
MAX_CHUNK = 8
G_QUAD = 4
Q_GROUP = 4
O_PAIR = 2
X_BUFS = 12
EARLY_Q = 0
E_AHEAD = 2
Y_ON_VECTOR = (3, 3, 3, 3, 2)
LATE_SQUARES = 1
DRAIN_FROM = 3

FLOPS = 2 * TOKENS * VOCAB * COLS
BYTES = TOKENS * VOCAB * (4 + 2) + VOCAB * (COLS - 1) * 2 + VOCAB * 8 + 2 + TOKENS * COLS * 4


def tile_geodesiclmheadv2_t_v_kernel(
    tc, hidden_states, weight, logit_scale, x, r, w_time, grad_out, out
):
    nc = tc.nc
    x_view = x.flatten_outer_dims().rearrange("(c p n) v -> c p n v", p=P, n=BLOCK)
    g_view = grad_out.flatten_outer_dims().rearrange("(c p n) v -> c p n v", p=P, n=BLOCK)
    out_view = out.flatten_outer_dims().rearrange("(c p n) w -> c p n w", p=P, n=BLOCK)

    with ExitStack() as stack:
        keep = stack.enter_context(tc.tile_pool(name="keep", bufs=1))
        x_pool = stack.enter_context(tc.tile_pool(name="x_pool", bufs=X_BUFS))
        g_pool = stack.enter_context(tc.tile_pool(name="g_pool", bufs=3))
        q_pool = stack.enter_context(tc.tile_pool(name="q_pool", bufs=MAX_CHUNK + 1))
        e_pool = stack.enter_context(tc.tile_pool(name="e_pool", bufs=MAX_CHUNK))
        d_pool = stack.enter_context(tc.tile_pool(name="d_pool", bufs=4))
        mx_pool = stack.enter_context(tc.tile_pool(name="mx_pool", bufs=2))
        o_pool = stack.enter_context(tc.tile_pool(name="o_pool", bufs=3))
        yt_psum = stack.enter_context(tc.psum_pool(name="yt_psum", bufs=2))
        bank_psum = stack.enter_context(tc.psum_pool(name="bank_psum", bufs=6))
        stack.enter_context(tc.manual_schedule())

        x_tiles = {}
        g_tiles = {}
        q_tiles = {}
        e_tiles = {}
        yt_tiles = {}
        et_tiles = {}
        gt_tiles = {}
        d_tiles = {}
        dx_tiles = {}
        code_tiles = {}
        acc_tiles = {}
        o_tiles = {}

        def load_x(i):
            if i >= TILES:
                return
            c, n = divmod(i, BLOCK)
            x_raw = x_pool.tile([P, VOCAB], F32, name="x_raw")
            nc.sync.dma_start(out=x_raw[:], in_=x_view[c, :, n, :])
            x_tiles[i] = x_raw

        def load_g(quad):
            if quad * G_QUAD >= TILES:
                return
            c, n = divmod(quad * G_QUAD, BLOCK)
            g_raw = g_pool.tile([P, G_QUAD, VOCAB], BF16, name="g_raw", align_bytes=64)
            nc.sync.dma_start(out=g_raw[:], in_=g_view[c, :, n : n + G_QUAD, :])
            g_tiles[quad] = g_raw

        for i in range(4):
            load_x(i)
        ls_sb = keep.tile([P, 1], BF16, name="ls_sb")
        nc.sync.dma_start(out=ls_sb[:], in_=logit_scale.partition_broadcast(P))
        r_sb = keep.tile([P, PASSES, PACK], F32, name="r_sb")
        wt_sb = keep.tile([P, PASSES, PACK], F32, name="wt_sb")
        with nc.allow_non_contiguous_dma(reason="16-byte runs of two small vectors"):
            nc.sync.dma_start(out=r_sb[:], in_=r.rearrange("(g p j) -> p g j", p=P, j=PACK))
            nc.sync.dma_start(out=wt_sb[:], in_=w_time.rearrange("(g p j) -> p g j", p=P, j=PACK))
        load_g(0)
        for i in range(4, 8):
            load_x(i)
        w_raw = g_pool.tile([P, PASSES, PACK, COLS - 1], BF16, name="w_raw", tag="g_raw", align_bytes=64)
        nc.sync.dma_start(out=w_raw[:], in_=weight.rearrange("(g p j) w -> p g j w", p=P, j=PACK))
        for i in range(8, X_BUFS):
            load_x(i)

        ident_f32 = keep.tile([P, P], F32, name="ident_f32")
        make_identity(nc, ident_f32[:])

        warm = keep.tile([P, 1], F32, name="warm")
        nc.vector.memset(warm[:], 1.0)
        nc.scalar.activation(out=warm[:], in_=warm[:], func=FUNC.Abs_reciprocal_sqrt)

        neg_r = keep.tile([P, PASSES, PACK], F32, name="neg_r")
        nc.gpsimd.tensor_scalar(
            out=neg_r[:], in0=r_sb[:], scalar1=-1.0, scalar2=0.0, op0=ALU.mult, op1=ALU.add
        )

        w_grp = g_pool.tile([P, PASSES, COLS, PACK], BF16, name="w_grp", tag="g_raw", align_bytes=64)
        w_codes = keep.tile([P, PASSES, COLS], U32, name="w_codes", align_bytes=64)
        w_scales = keep.tile([P, PASSES, COLS], U8, name="w_scales", align_bytes=64)
        def make_w(g):
            nc.gpsimd.tensor_copy(out=w_grp[:, g, 0, :], in_=wt_sb[:, g, :])
            nc.gpsimd.tensor_tensor(
                out=w_grp[:, g, 1:COLS, :],
                in0=w_raw[:, g].rearrange("p j w -> p w j"),
                in1=neg_r[:, g, :].unsqueeze(1).to_broadcast([P, COLS - 1, PACK]),
                op=ALU.mult,
            )

        def quantise_w(g):
            nc.vector.quantize_mx(
                out=w_codes[:, g, :].bitcast(E4M3_X4),
                scales=w_scales[:, g, :],
                in_=w_grp[:, g].rearrange("p w j -> p (w j)"),
            )

        def by_word(x_raw):
            return x_raw[:].rearrange("p (g c j) -> p g c j", g=PASSES, j=PACK)

        def square(i):
            if i >= TILES:
                return
            q_sb = q_pool.tile([P, PASSES, P, PACK], F32, name="q_sb")
            nc.scalar.activation(out=q_sb[:], in_=by_word(x_tiles[i]), func=FUNC.Square)
            q_tiles[i] = q_sb

        def square_on_vector(i):
            q_sb = q_pool.tile([P, PASSES, P, PACK], F32, name="q_sb")
            nc.vector.tensor_tensor(out=q_sb[:], in0=by_word(x_tiles[i]), in1=by_word(x_tiles[i]), op=ALU.mult)
            q_tiles[i] = q_sb

        def inverse_root(i):
            if i >= TILES:
                return
            e_sb = e_pool.tile([P, PASSES, P, PACK], F32, name="e_sb")
            nc.scalar.activation(
                out=e_sb[:], in_=q_tiles[i][:], func=FUNC.Abs_reciprocal_sqrt, bias=-1.0
            )
            e_tiles[i] = e_sb

        def root(i):
            if i >= TILES:
                return
            nc.vector.scalar_tensor_tensor(
                out=q_tiles[i][:], in0=q_tiles[i][:], scalar=-1.0, in1=e_tiles[i][:],
                op0=ALU.add, op1=ALU.mult,
            )

        def add_x(i, on_vector):
            x_raw = x_tiles.pop(i)
            if on_vector:
                nc.vector.tensor_tensor(
                    out=q_tiles[i][:], in0=by_word(x_raw), in1=q_tiles[i][:], op=ALU.add
                )
            else:
                nc.gpsimd.tensor_tensor(out=q_tiles[i][:], in0=by_word(x_raw), in1=q_tiles[i][:], op=ALU.add)
            load_x(i + X_BUFS)

        def transpose_y(i, g):
            yt = yt_psum.tile([P, PACK, P], F32, name="yt")
            for j in range(PACK):
                nc.tensor.transpose(yt[:, j, :], q_tiles[i][:, g, :, j], ident_f32[:])
            yt_tiles[i, g] = yt

        def transpose_e(i, g):
            et = bank_psum.tile([P, PACK, P], F32, name="et", tag="bank")
            for j in range(PACK):
                nc.tensor.transpose(et[:, j, :], e_tiles[i][:, g, :, j], ident_f32[:])
            et_tiles[i, g] = et

        def transpose_g(i):
            words = g_tiles[i // G_QUAD][:].bitcast(F32)
            cols = words[:, i % G_QUAD, :].rearrange("p (g c h) -> p g h c", g=PASSES, h=PACK // 2)
            gt = bank_psum.tile([P, PASSES, P, PACK // 2], F32, name="gt", tag="bank")
            for g in range(PASSES):
                for h in range(PACK // 2):
                    nc.tensor.transpose(gt[:, g, :, h], cols[:, g, h, :], ident_f32[:])
            gt_tiles[i] = gt
            if i % G_QUAD == G_QUAD - 1 and i > G_QUAD:
                load_g(i // G_QUAD + 3)

        def log(i, g):
            if g == 0:
                d_tiles[i] = d_pool.tile([P, PASSES, P, PACK], F32, name="d_sb")
            nc.scalar.activation(
                out=d_tiles[i][:, g], in_=yt_tiles.pop((i, g))[:].rearrange("p j t -> p t j"), func=FUNC.Ln
            )

        def times_e(i, g):
            nc.vector.scalar_tensor_tensor(
                out=d_tiles[i][:, g], in0=d_tiles[i][:, g], scalar=c_sb[:, 0:1],
                in1=et_tiles.pop((i, g))[:].rearrange("p j t -> p t j"),
                op0=ALU.mult, op1=ALU.mult,
            )

        def times_g(i):
            group, k = divmod(i, Q_GROUP)
            if k == 0:
                dx_tiles[group] = mx_pool.tile([P, Q_GROUP, VOCAB], BF16, name="dx", align_bytes=64)
            nc.vector.scalar_tensor_tensor(
                out=dx_tiles[group][:, k, :],
                in0=d_tiles.pop(i)[:].rearrange("p g t j -> p (g t j)"),
                scalar=0.0,
                in1=gt_tiles.pop(i)[:].rearrange("p g t h -> p (g t h)").bitcast(BF16),
                op0=ALU.min, op1=ALU.mult,
            )

        def quantise(group, k, count):
            if k == 0:
                codes = mx_pool.tile([P, Q_GROUP, PASSES, P], U32, name="codes", align_bytes=64)
                scales = mx_pool.tile([P, Q_GROUP, PASSES, P], U8, name="scales", align_bytes=64)
                code_tiles[group] = (codes, scales)
            codes, scales = code_tiles[group]
            nc.vector.quantize_mx(
                out=codes[:, k : k + count].rearrange("p k g t -> p (k g t)").bitcast(E5M2_X4),
                scales=scales[:, k : k + count].rearrange("p k g t -> p (k g t)"),
                in_=dx_tiles[group][:, k : k + count, :].rearrange("p k v -> p (k v)"),
            )

        def multiply(i):
            codes, scales = code_tiles[i // Q_GROUP]
            k = i % Q_GROUP
            acc = bank_psum.tile([P, COLS], F32, name="acc", tag="bank")
            for g in range(PASSES):
                nc.tensor.matmul_mx(
                    out=acc[:],
                    lhsT=codes[:, k, g, :].bitcast(E5M2_X4),
                    lhsT_scale=scales[:, k, g, :],
                    rhs=w_codes[:, g, :].bitcast(E4M3_X4),
                    rhs_scale=w_scales[:, g, :],
                    start=(g == 0),
                    stop=(g == PASSES - 1),
                )
            acc_tiles[i] = acc

        def drain(i, on_scalar):
            if i % O_PAIR == 0:
                o_tiles[i // O_PAIR] = o_pool.tile([P, O_PAIR, COLS], F32, name="o_sb")
            o_sb = o_tiles[i // O_PAIR]
            if on_scalar:
                nc.scalar.copy(out=o_sb[:, i % O_PAIR, :], in_=acc_tiles.pop(i)[:])
            else:
                nc.vector.tensor_copy(out=o_sb[:, i % O_PAIR, :], in_=acc_tiles.pop(i)[:])
            c, n = divmod(i, BLOCK)
            if i >= TILES - O_PAIR:
                nc.sync.dma_start(out=out_view[c, :, n, :], in_=o_sb[:, i % O_PAIR, :])
            elif i % O_PAIR == O_PAIR - 1:
                nc.sync.dma_start(out=out_view[c, :, n - (O_PAIR - 1) : n + 1, :], in_=o_sb[:])

        def chunk_order(c):
            on_vector = Y_ON_VECTOR[c]
            return list(range(on_vector)) + list(range(on_vector + 1, CHUNK_SIZES[c])) + [on_vector]

        def first_half(c, in_step):
            first, size = bounds[c], CHUNK_SIZES[c]
            waiting = []
            for k, n in enumerate(chunk_order(c)):
                if first + n not in q_tiles:
                    square(first + n)
                inverse_root(first + n)
                in_step(k)
                root(first + n)
                if waiting:
                    add_x(first + waiting.pop(0), True)
                if n < Y_ON_VECTOR[c]:
                    waiting.append(n)
            for n in range(Y_ON_VECTOR[c], size):
                add_x(first + n, False)

        def second_half(first, size, squares, after_product):
            per_step = -(-len(squares) // size)
            for g in range(PASSES):
                transpose_y(first, g)
            for i in range(first, first + E_AHEAD):
                for g in range(PASSES):
                    transpose_e(i, g)
            for n in range(size):
                i = first + n
                for g in range(PASSES):
                    log(i, g)
                    if n + 1 < size:
                        transpose_y(i + 1, g)
                transpose_g(i)
                if n + E_AHEAD < size:
                    for g in range(PASSES):
                        transpose_e(i + E_AHEAD, g)
                for j in squares[(n + 1) * per_step if n else 0 : (n + 2) * per_step]:
                    square(j)
                times_e(i, 0)
                times_e(i, 1)
                if n > 0:
                    times_g(i - 1)
                    after_product(i - 1)
            times_g(first + size - 1)
            after_product(first + size - 1)

        bounds = [sum(CHUNK_SIZES[:k]) for k in range(len(CHUNK_SIZES) + 1)]

        first_order = chunk_order(0)

        def squares_ahead(k):
            if k + 1 < CHUNK_SIZES[0]:
                if k == 0:
                    square_on_vector(first_order[k + 1])
                else:
                    square(first_order[k + 1])

        square(first_order[0])
        first_half(0, squares_ahead)
        for g in range(PASSES):
            make_w(g)
        c_sb = keep.tile([P, 1], F32, name="c_sb")
        nc.vector.tensor_scalar(
            out=c_sb[:], in0=ls_sb[:], scalar1=0.01, scalar2=2.5, op0=ALU.max, op1=ALU.min
        )
        nc.vector.tensor_scalar_mul(out=c_sb[:], in0=c_sb[:], scalar1=-2.0)

        for c, size in enumerate(CHUNK_SIZES):
            first = bounds[c]
            last_chunk = c + 1 == len(CHUNK_SIZES)
            after = 0 if last_chunk else CHUNK_SIZES[c + 1]
            def w_beside(i):
                if i == size - 1:
                    for g in range(PASSES):
                        quantise_w(g)
                    for quad in range(1, 4):
                        load_g(quad)

            def finish(i):
                if i > first:
                    quantise((i - 1) // Q_GROUP, (i - 1) % Q_GROUP, 1)
                if i > first + 1:
                    multiply(i - 2)
                if i > first + 2:
                    drain(i - 3, True)

            def early_groups(i):
                if i == first + Q_GROUP + EARLY_Q:
                    quantise(first // Q_GROUP, 0, Q_GROUP)

            ahead = [] if last_chunk else [first + size + n for n in chunk_order(c + 1)]
            if c == 0:
                ahead = ahead[: len(ahead) - LATE_SQUARES]
            second_half(
                first, size, sorted(ahead),
                w_beside if c == 0 else finish if last_chunk else early_groups,
            )
            if last_chunk:
                quantise((TILES - 1) // Q_GROUP, (TILES - 1) % Q_GROUP, 1)
                multiply(TILES - 2)
                drain(TILES - 3, True)
                multiply(TILES - 1)
                drain(TILES - 2, True)
                drain(TILES - 1, True)
            else:
                for group in range(first // Q_GROUP + (1 if c else 0), (first + size) // Q_GROUP):
                    quantise(group, 0, Q_GROUP)
                for n in range(size):
                    multiply(first + n)
                on_scalar = list(range(first, first + size * 3 // 4))

                def scalar_drains(k):
                    if k >= DRAIN_FROM and on_scalar:
                        drain(on_scalar.pop(0), True)

                first_half(c + 1, scalar_drains)
                while on_scalar:
                    drain(on_scalar.pop(0), True)
                for i in range(first + size * 3 // 4, first + size):
                    drain(i, False)
